import numpy as np
import ml_dtypes


def mxq(x, axis, fmt="e4m3"):
    dtype, down = {"e4m3": (ml_dtypes.float8_e4m3fn, 7), "e5m2": (ml_dtypes.float8_e5m2, 14)}[fmt]
    v = np.moveaxis(np.asarray(x, np.float32).astype(ml_dtypes.bfloat16).astype(np.float64), axis, -1)
    blocks = v.reshape(v.shape[:-1] + (-1, 32))
    amax = np.abs(blocks).max(-1, keepdims=True)
    byte = np.maximum(np.where(amax > 0, np.frexp(amax)[1] - 1 + 127, 0) - down, 1)
    scale = np.exp2(byte - 127.0)
    codes = (blocks / scale).astype(np.float32).astype(dtype).astype(np.float64)
    return np.moveaxis((codes * scale).reshape(v.shape), -1, axis)


WIDE = False


def mx_kscale(k):
    if not WIDE:
        return np.ones(k)
    levels = np.array([10, -10, 5, -5, 0])
    a = np.random.permutation(np.resize(levels, k // 512 * 4)).reshape(k // 512, 4)
    idx = np.arange(k)
    return np.exp2(a[idx // 512, idx % 128 // 32])


BF16 = ml_dtypes.bfloat16


def bf(x):
    return np.asarray(x, np.float32).astype(BF16)


def f64(x):
    return np.asarray(x).astype(np.float64)


E2M1 = np.array([0.0, 0.5, 1.0, 1.5, 2.0, 3.0, 4.0, 6.0, -0.0, -0.5, -1.0, -1.5, -2.0, -3.0, -4.0, -6.0])


def pack_weight(w, fmt):
    k, n = w.shape
    w = f64(bf(w)).reshape(k // 32, 32, n)
    amax = np.abs(w).max(1)
    if fmt == "e4m3":
        byte = np.frexp(amax)[1] - 1 + 127 - 7
    else:
        mant, ex = np.frexp(amax / 6.0)
        byte = np.where(mant > 0.5, ex, ex - 1) + 127
    byte = np.clip(np.where(amax > 0, byte, 1), 1, 254)
    scaled = (w * np.exp2(127.0 - byte)[:, None, :]).reshape(k, n).astype(np.float32)
    by_word = np.ascontiguousarray(scaled.reshape(k // 512, 128, 4, n).transpose(0, 1, 3, 2))
    if fmt == "e4m3":
        words = by_word.astype(ml_dtypes.float8_e4m3fn).view(np.uint8)
    else:
        c = by_word.astype(ml_dtypes.float4_e2m1fn).view(np.uint8) & 0xF
        words = c[..., 0::2] | (c[..., 1::2] << 4)
    return np.ascontiguousarray(words), np.ascontiguousarray(byte.astype(np.uint8).reshape(k // 512, 16, n))


def unpack_weight(words, scales, fmt):
    g, p, n, _ = words.shape
    if fmt == "e4m3":
        vals = np.ascontiguousarray(words).view(ml_dtypes.float8_e4m3fn).astype(np.float64)
    else:
        nib = np.empty((g, p, n, 4), np.uint8)
        nib[..., 0::2] = words & 0xF
        nib[..., 1::2] = words >> 4
        vals = E2M1[nib]
    vals = vals * np.repeat(np.exp2(scales.astype(np.float64) - 127.0), 8, axis=1)[..., None]
    return vals.transpose(0, 1, 3, 2).reshape(g * 512, n)


B, D_IN, D_HID, SHARE = 1024, 512, 256, 2
NUM_GATE = 4 + SHARE


def sigmoid(v):
    return 1.0 / (1.0 + np.exp(-v))


def setup_inputs():
    s = mx_kscale(D_IN)
    n = np.random.standard_normal
    inp = bf(n((B, D_IN)) * s)
    h_minors = bf(n((B, D_HID)))
    c_minors = bf(n((B, D_HID)))
    s_minors = bf(n((SHARE, B, D_HID)))
    mask = bf(np.random.uniform(0.5, 1.5, B))
    w_ih = n((NUM_GATE * D_HID, D_IN)) * 0.7 / np.sqrt(D_IN) / s
    words, scales = pack_weight(np.ascontiguousarray(w_ih.T), "e4m3")
    return {
        "input": inp,
        "h_minors": h_minors,
        "c_minors": c_minors,
        "s_minors": s_minors,
        "mask": mask,
        "weight_ih_words": words,
        "weight_ih_scales": scales,
        "weight_hh": bf(n((4 * D_HID, D_HID)) * 0.7 / np.sqrt(D_HID)),
        "weight_sh": bf(n((SHARE * D_HID, D_HID)) * 0.7 / np.sqrt(D_HID)),
        "bias_ih": bf(n(NUM_GATE * D_HID) * 0.3),
        "bias_hh": bf(n(4 * D_HID) * 0.3),
        "bias_sh": bf(n(SHARE * D_HID) * 0.3),
        "idx": 0,
    }


def reference(input, h_minors, c_minors, s_minors, mask, weight_ih_words, weight_ih_scales, weight_hh, weight_sh, bias_ih, bias_hh, bias_sh, idx):
    H = weight_hh.shape[1]
    share = weight_sh.shape[0] // H
    m = f64(mask)[:, None]
    tmp = (mxq(f64(input), 1, "e4m3") @ unpack_weight(weight_ih_words, weight_ih_scales, "e4m3")) + f64(bias_ih)
    tmp2 = f64(h_minors) @ f64(weight_hh).T + f64(bias_hh)
    tmp3 = f64(s_minors)[idx] @ f64(weight_sh).T + f64(bias_sh)
    tmp_in, tmp_s = tmp[:, :4 * H], tmp[:, 4 * H:]
    z = tmp_in + tmp2
    ifo = sigmoid(z[:, :3 * H])
    i, f, o = ifo[:, :H], ifo[:, H:2 * H], ifo[:, 2 * H:]
    c_hat = z[:, 3 * H:]
    b = sigmoid(tmp_s + tmp3)
    c_t = (f * f64(c_minors) + i * np.tanh(c_hat)) * m
    tc = np.tanh(c_t) * m
    h = o * tc
    s = b.reshape(-1, share, H) * tc[:, None, :]
    s = np.moveaxis(s, 1, 0)
    return (h, c_t, s[0], s[1])

@@ -1,0 +1,240 @@
+from contextlib import ExitStack
+
+import concourse.mybir as mybir
+from concourse.masks import make_identity
+
+F32 = mybir.dt.float32
+BF16 = mybir.dt.bfloat16
+I32 = mybir.dt.int32
+U32 = mybir.dt.uint32
+U8 = mybir.dt.uint8
+FP8X4 = mybir.dt.float8_e4m3fn_x4
+ACT = mybir.ActivationFunctionType
+ALU = mybir.AluOpType
+
+P = 128
+BATCH, D_IN, HID = 1024, 512, 256
+GATES = 6 * HID
+ROW_TILES = BATCH // P
+HALF = ROW_TILES // 2
+CHUNK = 512
+N_CHUNKS = GATES // CHUNK
+PER_BANK = CHUNK // P
+
+FLOPS = 2 * BATCH * (D_IN * GATES + HID * 4 * HID + HID * 2 * HID)
+
+
+def tile_share_lstm_cell_kernel(
+    tc,
+    x,
+    h_minors,
+    c_minors,
+    s_minors,
+    mask,
+    weight_ih_words,
+    weight_ih_scales,
+    weight_hh,
+    weight_sh,
+    bias_ih,
+    bias_hh,
+    bias_sh,
+    idx,
+    out_0,
+    out_1,
+    out_2,
+    out_3,
+):
+    nc = tc.nc
+    with ExitStack() as stack:
+        keep = stack.enter_context(tc.tile_pool(name="keep", bufs=1))
+        work = stack.enter_context(tc.tile_pool(name="work", bufs=3))
+        banks = stack.enter_context(tc.psum_pool(name="banks", bufs=8))
+
+        bias_rows = keep.tile([P, GATES], BF16)
+        nc.vector.memset(bias_rows[:].bitcast(I32), 0)
+        nc.scalar.dma_start(out=bias_rows[0:1, :], in_=bias_ih.rearrange("(o n) -> o n", o=1))
+        nc.scalar.dma_start(
+            out=bias_rows[1:2, 0 : 4 * HID], in_=bias_hh.rearrange("(o n) -> o n", o=1)
+        )
+        nc.scalar.dma_start(
+            out=bias_rows[1:2, 4 * HID : GATES], in_=bias_sh.rearrange("(o n) -> o n", o=1)
+        )
+        ones = keep.tile([P, P], BF16)
+        nc.vector.memset(ones[:], 1.0)
+
+        w_plane = keep.tile([P, GATES], U8, align_bytes=64)
+        nc.vector.memset(w_plane[:].bitcast(I32), 0)
+
+        warm = keep.tile([P, 1], F32)
+        nc.vector.memset(warm[:], 0.0)
+        nc.scalar.activation(out=warm[:], in_=warm[:], func=ACT.Sigmoid)
+
+        ident = keep.tile([P, P], F32)
+        make_identity(nc, ident[:])
+
+        x_sb = keep.tile([P, ROW_TILES, D_IN], BF16)
+        state_sb = keep.tile([P, 2, ROW_TILES, HID], BF16)
+        c_sb = keep.tile([P, ROW_TILES, HID], BF16)
+        rec_sb = keep.tile([P, GATES // P, HID], BF16)
+        w_words = keep.tile([P, GATES], U32, align_bytes=64)
+        mask_bf = keep.tile([P, ROW_TILES], BF16)
+
+        x_rows = x.rearrange("(p r) k -> p r k", r=ROW_TILES)
+        h_rows = h_minors.rearrange("(p r) k -> p r k", r=ROW_TILES)
+        s_rows = s_minors[idx].rearrange("(p r) k -> p r k", r=ROW_TILES)
+        hh_rows = weight_hh.rearrange("(t p) k -> p t k", p=P)
+        sh_rows = weight_sh.rearrange("(t p) k -> p t k", p=P)
+        words_i32 = weight_ih_words[0].rearrange("p n t -> p (n t)").bitcast(I32)
+        scales_i32 = weight_ih_scales[0].bitcast(I32)
+
+        def load_w_words(j):
+            cols = slice(j * CHUNK, (j + 1) * CHUNK)
+            nc.sync.dma_start(out=w_words[:, cols].bitcast(I32), in_=words_i32[:, cols])
+
+        first, second = slice(0, HALF), slice(HALF, ROW_TILES)
+        nc.sync.dma_start(out=x_sb[:, first, :], in_=x_rows[:, first, :])
+        nc.sync.dma_start(out=rec_sb[:, 0:4, :], in_=hh_rows[:, 0:4, :])
+        nc.sync.dma_start(out=state_sb[:, 0, first, :], in_=h_rows[:, first, :])
+        for quad in range(4):
+            nc.sync.dma_start(
+                out=w_plane[32 * quad : 32 * quad + 4, :].bitcast(I32),
+                in_=scales_i32[4 * quad : 4 * quad + 4, :],
+            )
+        load_w_words(0)
+        nc.sync.dma_start(out=rec_sb[:, 4:8, :], in_=hh_rows[:, 4:8, :])
+        load_w_words(1)
+        nc.sync.dma_start(out=rec_sb[:, 8:12, :], in_=sh_rows)
+        nc.sync.dma_start(out=state_sb[:, 1, first, :], in_=s_rows[:, first, :])
+        load_w_words(2)
+        nc.sync.dma_start(out=mask_bf[:], in_=mask.rearrange("(p r) -> p r", r=ROW_TILES))
+        nc.sync.dma_start(out=c_sb[:], in_=c_minors.rearrange("(p r) k -> p r k", r=ROW_TILES))
+        nc.sync.dma_start(out=x_sb[:, second, :], in_=x_rows[:, second, :])
+        nc.sync.dma_start(out=state_sb[:, 0, second, :], in_=h_rows[:, second, :])
+        nc.sync.dma_start(out=state_sb[:, 1, second, :], in_=s_rows[:, second, :])
+
+        mask_f = keep.tile([P, ROW_TILES], F32)
+        nc.vector.tensor_copy(out=mask_f[:], in_=mask_bf[:])
+
+        x_words = x_sb[:].bitcast(F32)
+        state_words = state_sb[:].bitcast(F32)
+        rec_words = rec_sb[:].bitcast(F32)
+
+        x_grouped = keep.tile([P, ROW_TILES, 4 * P], BF16, align_bytes=64)
+        x_codes = keep.tile([P, ROW_TILES * P], U32, align_bytes=64)
+        x_plane = keep.tile([P, ROW_TILES * P], U8, align_bytes=64)
+        stateT = keep.tile([P, 2, ROW_TILES, P], F32)
+        recT = keep.tile([P, GATES], F32)
+        bias_all = keep.tile([P, GATES], F32)
+
+        def prepare_rows(start):
+            pairs = range(start, start + HALF, 2)
+            for pair in pairs:
+                bank = banks.tile([P, PER_BANK, P], F32, tag="bank")
+                for r in range(2):
+                    for u in range(2):
+                        nc.tensor.transpose(
+                            bank[:, 2 * r + u, :], x_words[:, pair + r, u : D_IN // 2 : 2], ident[:]
+                        )
+                nc.vector.tensor_copy(
+                    out=x_grouped[:, pair : pair + 2, :]
+                    .bitcast(F32)
+                    .rearrange("p r (b u) -> p r b u", u=2),
+                    in_=bank[:].rearrange("p (r u) b -> p r b u", u=2),
+                )
+            for pair in pairs:
+                cols = slice(pair * P, (pair + 2) * P)
+                nc.vector.quantize_mx(
+                    out=x_codes[:, cols].bitcast(FP8X4),
+                    scales=x_plane[:, cols],
+                    in_=x_grouped[:, pair : pair + 2, :].rearrange("p r c -> p (r c)"),
+                )
+            for which in range(2):
+                bank = banks.tile([P, PER_BANK, P], F32, tag="bank")
+                for q in range(HALF):
+                    nc.tensor.transpose(
+                        bank[:, q, :], state_words[:, which, start + q, :], ident[:]
+                    )
+                nc.scalar.copy(out=stateT[:, which, start : start + HALF, :], in_=bank[:])
+
+        def prepare_chunk(j):
+            cols = slice(j * CHUNK, (j + 1) * CHUNK)
+            bank = banks.tile([P, PER_BANK, P], F32, tag="bank")
+            for q in range(PER_BANK):
+                nc.tensor.transpose(bank[:, q, :], rec_words[:, PER_BANK * j + q, :], ident[:])
+            nc.scalar.copy(out=recT[:, cols], in_=bank[:].rearrange("p q n -> p (q n)"))
+            bias_sum = banks.tile([P, CHUNK], F32, tag="bank")
+            nc.tensor.matmul(out=bias_sum[:], lhsT=ones[:], rhs=bias_rows[:, cols], start=True, stop=True)
+            nc.scalar.copy(out=bias_all[:, cols], in_=bias_sum[:])
+
+        stateT_bf = stateT[:].bitcast(BF16)
+        recT_bf = recT[:].bitcast(BF16)
+
+        out_rows = [o.rearrange("(p r) c -> p r c", r=ROW_TILES) for o in (out_1, out_0, out_2, out_3)]
+
+        def cell(r):
+            m = mask_f[:, r : r + 1]
+            z = work.tile([P, GATES], F32)
+            for j in range(N_CHUNKS):
+                cols = slice(j * CHUNK, (j + 1) * CHUNK)
+                mx_sum = banks.tile([P, CHUNK], F32, tag="bank")
+                nc.tensor.matmul_mx(
+                    out=mx_sum[:],
+                    lhsT=x_codes[:, r * P : (r + 1) * P].bitcast(FP8X4),
+                    lhsT_scale=x_plane[:, r * P : (r + 1) * P],
+                    rhs=w_words[:, cols].bitcast(FP8X4),
+                    rhs_scale=w_plane[:, cols],
+                    start=True,
+                    stop=True,
+                )
+                which = j // 2
+                plain_sum = banks.tile([P, CHUNK], F32, tag="bank")
+                for e in range(2):
+                    nc.tensor.matmul(
+                        out=plain_sum[:],
+                        lhsT=stateT_bf[:, which, r, e : 2 * P : 2],
+                        rhs=recT_bf[:, 2 * j * CHUNK + e : 2 * (j + 1) * CHUNK : 2],
+                        start=(e == 0),
+                        stop=(e == 1),
+                    )
+                nc.vector.tensor_tensor(out=z[:, cols], in0=plain_sum[:], in1=bias_all[:, cols], op=ALU.add)
+                nc.vector.tensor_tensor(out=z[:, cols], in0=mx_sum[:], in1=z[:, cols], op=ALU.add)
+
+            gates = work.tile([P, 5, HID], F32)
+            flat = gates[:].rearrange("p g c -> p (g c)")
+            g_hat = work.tile([P, HID], F32)
+            nc.scalar.activation(out=flat[:, 0 : 2 * HID], in_=z[:, 0 : 2 * HID], func=ACT.Sigmoid)
+            nc.scalar.activation(out=flat[:, 2 * HID : 3 * HID], in_=z[:, 2 * HID : 3 * HID], func=ACT.Sigmoid)
+            nc.scalar.activation(out=g_hat[:], in_=z[:, 3 * HID : 4 * HID], func=ACT.Tanh)
+            nc.scalar.activation(out=flat[:, 3 * HID : 5 * HID], in_=z[:, 4 * HID : 6 * HID], func=ACT.Sigmoid)
+
+            res = work.tile([P, 4, HID], F32)
+            keep_part = work.tile([P, HID], F32)
+            new_part = work.tile([P, HID], F32)
+            nc.vector.scalar_tensor_tensor(
+                out=keep_part[:], in0=gates[:, 1, :], scalar=m, in1=c_sb[:, r, :], op0=ALU.mult, op1=ALU.mult
+            )
+            nc.vector.scalar_tensor_tensor(
+                out=new_part[:], in0=gates[:, 0, :], scalar=m, in1=g_hat[:], op0=ALU.mult, op1=ALU.mult
+            )
+            nc.vector.tensor_tensor(out=res[:, 0, :], in0=keep_part[:], in1=new_part[:], op=ALU.add)
+            tanh_c = work.tile([P, HID], F32)
+            nc.scalar.activation(out=tanh_c[:], in_=res[:, 0, :], func=ACT.Tanh)
+            nc.vector.scalar_tensor_tensor(
+                out=res[:, 1:4, :],
+                in0=gates[:, 2:5, :],
+                scalar=m,
+                in1=tanh_c[:].unsqueeze(1).to_broadcast([P, 3, HID]),
+                op0=ALU.mult,
+                op1=ALU.mult,
+            )
+            for k in range(4):
+                nc.sync.dma_start(out=out_rows[k][:, r, :], in_=res[:, k, :])
+
+        prepare_rows(0)
+        for j in range(N_CHUNKS):
+            prepare_chunk(j)
+        for r in range(0, HALF):
+            cell(r)
+        prepare_rows(HALF)
+        for r in range(HALF, ROW_TILES):
+            cell(r)

@@ -15,11 +15,14 @@ ALU = mybir.AluOpType
 P = 128
 BATCH, D_IN, HID = 1024, 512, 256
 GATES = 6 * HID
+GATE_TILES = GATES // P
 ROW_TILES = BATCH // P
-HALF = ROW_TILES // 2
 CHUNK = 512
 N_CHUNKS = GATES // CHUNK
 PER_BANK = CHUNK // P
+HALF = CHUNK // P
+PREPARE_AFTER = 0
+MULTIPLY_AFTER = 2
 
 FLOPS = 2 * BATCH * (D_IN * GATES + HID * 4 * HID + HID * 2 * HID)
 
@@ -49,33 +52,25 @@ def tile_share_lstm_cell_kernel(
         keep = stack.enter_context(tc.tile_pool(name="keep", bufs=1))
         work = stack.enter_context(tc.tile_pool(name="work", bufs=3))
         banks = stack.enter_context(tc.psum_pool(name="banks", bufs=8))
+        stack.enter_context(tc.manual_schedule())
 
-        bias_rows = keep.tile([P, GATES], BF16)
+        bias_rows = keep.tile([P, 2, P], BF16)
         nc.vector.memset(bias_rows[:].bitcast(I32), 0)
-        nc.scalar.dma_start(out=bias_rows[0:1, :], in_=bias_ih.rearrange("(o n) -> o n", o=1))
-        nc.scalar.dma_start(
-            out=bias_rows[1:2, 0 : 4 * HID], in_=bias_hh.rearrange("(o n) -> o n", o=1)
-        )
-        nc.scalar.dma_start(
-            out=bias_rows[1:2, 4 * HID : GATES], in_=bias_sh.rearrange("(o n) -> o n", o=1)
-        )
-        ones = keep.tile([P, P], BF16)
-        nc.vector.memset(ones[:], 1.0)
-
+        nc.scalar.dma_start(out=bias_rows[0:GATE_TILES, 0, :], in_=bias_ih.rearrange("(g n) -> g n", n=P))
+        nc.scalar.dma_start(out=bias_rows[0:8, 1, :], in_=bias_hh.rearrange("(g n) -> g n", n=P))
+        nc.scalar.dma_start(out=bias_rows[8:GATE_TILES, 1, :], in_=bias_sh.rearrange("(g n) -> g n", n=P))
         w_plane = keep.tile([P, GATES], U8, align_bytes=64)
         nc.vector.memset(w_plane[:].bitcast(I32), 0)
-
         warm = keep.tile([P, 1], F32)
         nc.vector.memset(warm[:], 0.0)
         nc.scalar.activation(out=warm[:], in_=warm[:], func=ACT.Sigmoid)
-
         ident = keep.tile([P, P], F32)
         make_identity(nc, ident[:])
 
         x_sb = keep.tile([P, ROW_TILES, D_IN], BF16)
         state_sb = keep.tile([P, 2, ROW_TILES, HID], BF16)
         c_sb = keep.tile([P, ROW_TILES, HID], BF16)
-        rec_sb = keep.tile([P, GATES // P, HID], BF16)
+        rec_sb = keep.tile([P, GATE_TILES, HID], BF16)
         w_words = keep.tile([P, GATES], U32, align_bytes=64)
         mask_bf = keep.tile([P, ROW_TILES], BF16)
 
@@ -87,33 +82,40 @@ def tile_share_lstm_cell_kernel(
         words_i32 = weight_ih_words[0].rearrange("p n t -> p (n t)").bitcast(I32)
         scales_i32 = weight_ih_scales[0].bitcast(I32)
 
+        def load_x(q):
+            rows = slice(2 * q, 2 * q + 2)
+            nc.sync.dma_start(out=x_sb[:, rows, :], in_=x_rows[:, rows, :])
+
+        def load_state(q):
+            rows = slice(2 * q, 2 * q + 2)
+            nc.sync.dma_start(out=state_sb[:, 0, rows, :], in_=h_rows[:, rows, :])
+            nc.sync.dma_start(out=state_sb[:, 1, rows, :], in_=s_rows[:, rows, :])
+
         def load_w_words(j):
             cols = slice(j * CHUNK, (j + 1) * CHUNK)
             nc.sync.dma_start(out=w_words[:, cols].bitcast(I32), in_=words_i32[:, cols])
 
-        first, second = slice(0, HALF), slice(HALF, ROW_TILES)
-        nc.sync.dma_start(out=x_sb[:, first, :], in_=x_rows[:, first, :])
+        nc.gpsimd.dma_start(out=mask_bf[:], in_=mask.rearrange("(p r) -> p r", r=ROW_TILES))
+        load_x(0)
+        load_x(1)
         nc.sync.dma_start(out=rec_sb[:, 0:4, :], in_=hh_rows[:, 0:4, :])
-        nc.sync.dma_start(out=state_sb[:, 0, first, :], in_=h_rows[:, first, :])
         for quad in range(4):
             nc.sync.dma_start(
                 out=w_plane[32 * quad : 32 * quad + 4, :].bitcast(I32),
                 in_=scales_i32[4 * quad : 4 * quad + 4, :],
             )
         load_w_words(0)
-        nc.sync.dma_start(out=rec_sb[:, 4:8, :], in_=hh_rows[:, 4:8, :])
         load_w_words(1)
-        nc.sync.dma_start(out=rec_sb[:, 8:12, :], in_=sh_rows)
-        nc.sync.dma_start(out=state_sb[:, 1, first, :], in_=s_rows[:, first, :])
         load_w_words(2)
-        nc.sync.dma_start(out=mask_bf[:], in_=mask.rearrange("(p r) -> p r", r=ROW_TILES))
+        load_state(0)
+        nc.sync.dma_start(out=rec_sb[:, 4:8, :], in_=hh_rows[:, 4:8, :])
+        nc.sync.dma_start(out=rec_sb[:, 8:12, :], in_=sh_rows)
+        load_state(1)
         nc.sync.dma_start(out=c_sb[:], in_=c_minors.rearrange("(p r) k -> p r k", r=ROW_TILES))
-        nc.sync.dma_start(out=x_sb[:, second, :], in_=x_rows[:, second, :])
-        nc.sync.dma_start(out=state_sb[:, 0, second, :], in_=h_rows[:, second, :])
-        nc.sync.dma_start(out=state_sb[:, 1, second, :], in_=s_rows[:, second, :])
-
-        mask_f = keep.tile([P, ROW_TILES], F32)
-        nc.vector.tensor_copy(out=mask_f[:], in_=mask_bf[:])
+        load_x(2)
+        load_x(3)
+        load_state(2)
+        load_state(3)
 
         x_words = x_sb[:].bitcast(F32)
         state_words = state_sb[:].bitcast(F32)
@@ -124,90 +126,117 @@ def tile_share_lstm_cell_kernel(
         x_plane = keep.tile([P, ROW_TILES * P], U8, align_bytes=64)
         stateT = keep.tile([P, 2, ROW_TILES, P], F32)
         recT = keep.tile([P, GATES], F32)
-        bias_all = keep.tile([P, GATES], F32)
-
-        def prepare_rows(start):
-            pairs = range(start, start + HALF, 2)
-            for pair in pairs:
-                bank = banks.tile([P, PER_BANK, P], F32, tag="bank")
-                for r in range(2):
-                    for u in range(2):
-                        nc.tensor.transpose(
-                            bank[:, 2 * r + u, :], x_words[:, pair + r, u : D_IN // 2 : 2], ident[:]
-                        )
-                nc.vector.tensor_copy(
-                    out=x_grouped[:, pair : pair + 2, :]
-                    .bitcast(F32)
-                    .rearrange("p r (b u) -> p r b u", u=2),
-                    in_=bank[:].rearrange("p (r u) b -> p r b u", u=2),
-                )
-            for pair in pairs:
-                cols = slice(pair * P, (pair + 2) * P)
-                nc.vector.quantize_mx(
-                    out=x_codes[:, cols].bitcast(FP8X4),
-                    scales=x_plane[:, cols],
-                    in_=x_grouped[:, pair : pair + 2, :].rearrange("p r c -> p (r c)"),
-                )
-            for which in range(2):
-                bank = banks.tile([P, PER_BANK, P], F32, tag="bank")
-                for q in range(HALF):
-                    nc.tensor.transpose(
-                        bank[:, q, :], state_words[:, which, start + q, :], ident[:]
-                    )
-                nc.scalar.copy(out=stateT[:, which, start : start + HALF, :], in_=bank[:])
-
-        def prepare_chunk(j):
-            cols = slice(j * CHUNK, (j + 1) * CHUNK)
-            bank = banks.tile([P, PER_BANK, P], F32, tag="bank")
-            for q in range(PER_BANK):
-                nc.tensor.transpose(bank[:, q, :], rec_words[:, PER_BANK * j + q, :], ident[:])
-            nc.scalar.copy(out=recT[:, cols], in_=bank[:].rearrange("p q n -> p (q n)"))
-            bias_sum = banks.tile([P, CHUNK], F32, tag="bank")
-            nc.tensor.matmul(out=bias_sum[:], lhsT=ones[:], rhs=bias_rows[:, cols], start=True, stop=True)
-            nc.scalar.copy(out=bias_all[:, cols], in_=bias_sum[:])
-
         stateT_bf = stateT[:].bitcast(BF16)
         recT_bf = recT[:].bitcast(BF16)
+        bias_col = keep.tile([P, GATE_TILES], F32)
+        mask_f = keep.tile([P, ROW_TILES], F32)
+        mxT = keep.tile([P, ROW_TILES // HALF, GATE_TILES, CHUNK], F32)
 
-        out_rows = [o.rearrange("(p r) c -> p r c", r=ROW_TILES) for o in (out_1, out_0, out_2, out_3)]
+        def transpose_bias():
+            bias_gn = keep.tile([P, P], F32)
+            nc.vector.tensor_tensor(out=bias_gn[:], in0=bias_rows[:, 0, :], in1=bias_rows[:, 1, :], op=ALU.add)
+            bias_bank = banks.tile([P, P], F32, tag="bank")
+            nc.tensor.transpose(bias_bank[:], bias_gn[:], ident[:])
+            nc.vector.tensor_copy(out=bias_col[:], in_=bias_bank[:, 0:GATE_TILES])
 
-        def cell(r):
-            m = mask_f[:, r : r + 1]
-            z = work.tile([P, GATES], F32)
-            for j in range(N_CHUNKS):
-                cols = slice(j * CHUNK, (j + 1) * CHUNK)
-                mx_sum = banks.tile([P, CHUNK], F32, tag="bank")
+        def transpose_x(q):
+            x_bank = banks.tile([P, PER_BANK, P], F32, tag="bank")
+            for r in range(2):
+                for u in range(2):
+                    nc.tensor.transpose(
+                        x_bank[:, 2 * r + u, :], x_words[:, 2 * q + r, u : D_IN // 2 : 2], ident[:]
+                    )
+            side_by_side = x_grouped[:, 2 * q : 2 * q + 2, :].bitcast(F32).rearrange("p r (b u) -> p r b u", u=2)
+            by_word = x_bank[:].rearrange("p (r u) b -> p r b u", u=2)
+            if q % 2 == 0:
+                nc.vector.tensor_copy(out=side_by_side, in_=by_word)
+            else:
+                nc.scalar.copy(out=side_by_side, in_=by_word)
+
+        def quantise_x(q):
+            cols = slice(2 * q * P, (2 * q + 2) * P)
+            nc.vector.quantize_mx(
+                out=x_codes[:, cols].bitcast(FP8X4),
+                scales=x_plane[:, cols],
+                in_=x_grouped[:, 2 * q : 2 * q + 2, :].rearrange("p r c -> p (r c)"),
+            )
+
+        def transpose_state(q):
+            state_bank = banks.tile([P, PER_BANK, P], F32, tag="bank")
+            for which in range(2):
+                for r in range(2):
+                    nc.tensor.transpose(
+                        state_bank[:, 2 * which + r, :], state_words[:, which, 2 * q + r, :], ident[:]
+                    )
+            nc.vector.tensor_copy(
+                out=stateT[:, :, 2 * q : 2 * q + 2, :], in_=state_bank[:].rearrange("p (w r) b -> p w r b", r=2)
+            )
+
+        def transpose_weights(j):
+            rec_bank = banks.tile([P, PER_BANK, P], F32, tag="bank")
+            for t in range(PER_BANK):
+                nc.tensor.transpose(rec_bank[:, t, :], rec_words[:, PER_BANK * j + t, :], ident[:])
+            nc.scalar.copy(
+                out=recT[:, j * CHUNK : (j + 1) * CHUNK], in_=rec_bank[:].rearrange("p t n -> p (t n)")
+            )
+
+        def mx_transposed(half):
+            rows = slice(half * CHUNK, (half + 1) * CHUNK)
+            for g in range(GATE_TILES):
+                cols = slice(g * P, (g + 1) * P)
+                mx_bank = banks.tile([P, CHUNK], F32, tag="bank")
                 nc.tensor.matmul_mx(
-                    out=mx_sum[:],
-                    lhsT=x_codes[:, r * P : (r + 1) * P].bitcast(FP8X4),
-                    lhsT_scale=x_plane[:, r * P : (r + 1) * P],
-                    rhs=w_words[:, cols].bitcast(FP8X4),
-                    rhs_scale=w_plane[:, cols],
+                    out=mx_bank[:],
+                    lhsT=w_words[:, cols].bitcast(FP8X4),
+                    lhsT_scale=w_plane[:, cols],
+                    rhs=x_codes[:, rows].bitcast(FP8X4),
+                    rhs_scale=x_plane[:, rows],
                     start=True,
                     stop=True,
                 )
-                which = j // 2
-                plain_sum = banks.tile([P, CHUNK], F32, tag="bank")
+                if g % 2 == 0:
+                    nc.vector.tensor_scalar_add(out=mxT[:, half, g, :], in0=mx_bank[:], scalar1=bias_col[:, g : g + 1])
+                else:
+                    nc.scalar.activation(
+                        out=mxT[:, half, g, :], in_=mx_bank[:], func=ACT.Identity, bias=bias_col[:, g : g + 1]
+                    )
+
+        def arguments(r):
+            z_banks = []
+            for j in range(N_CHUNKS):
+                z_bank = banks.tile([P, CHUNK], F32, tag="bank")
                 for e in range(2):
                     nc.tensor.matmul(
-                        out=plain_sum[:],
-                        lhsT=stateT_bf[:, which, r, e : 2 * P : 2],
+                        out=z_bank[:],
+                        lhsT=stateT_bf[:, j // 2, r, e : 2 * P : 2],
                         rhs=recT_bf[:, 2 * j * CHUNK + e : 2 * (j + 1) * CHUNK : 2],
                         start=(e == 0),
-                        stop=(e == 1),
+                        stop=False,
                     )
-                nc.vector.tensor_tensor(out=z[:, cols], in0=plain_sum[:], in1=bias_all[:, cols], op=ALU.add)
-                nc.vector.tensor_tensor(out=z[:, cols], in0=mx_sum[:], in1=z[:, cols], op=ALU.add)
+                for t in range(PER_BANK):
+                    nc.tensor.matmul(
+                        out=z_bank[:, t * P : (t + 1) * P],
+                        lhsT=mxT[:, r // HALF, PER_BANK * j + t, (r % HALF) * P : (r % HALF + 1) * P],
+                        rhs=ident[:],
+                        is_transpose=True,
+                        start=False,
+                        stop=(t == PER_BANK - 1),
+                    )
+                z_banks.append(z_bank)
+            return z_banks
 
+        def functions(z_banks):
             gates = work.tile([P, 5, HID], F32)
-            flat = gates[:].rearrange("p g c -> p (g c)")
             g_hat = work.tile([P, HID], F32)
-            nc.scalar.activation(out=flat[:, 0 : 2 * HID], in_=z[:, 0 : 2 * HID], func=ACT.Sigmoid)
-            nc.scalar.activation(out=flat[:, 2 * HID : 3 * HID], in_=z[:, 2 * HID : 3 * HID], func=ACT.Sigmoid)
-            nc.scalar.activation(out=g_hat[:], in_=z[:, 3 * HID : 4 * HID], func=ACT.Tanh)
-            nc.scalar.activation(out=flat[:, 3 * HID : 5 * HID], in_=z[:, 4 * HID : 6 * HID], func=ACT.Sigmoid)
+            flat = gates[:].rearrange("p g c -> p (g c)")
+            nc.scalar.activation(out=flat[:, 0 : 2 * HID], in_=z_banks[0][:], func=ACT.Sigmoid)
+            nc.scalar.activation(out=g_hat[:], in_=z_banks[1][:, HID : 2 * HID], func=ACT.Tanh)
+            nc.scalar.activation(out=flat[:, 2 * HID : 3 * HID], in_=z_banks[1][:, 0:HID], func=ACT.Sigmoid)
+            nc.scalar.activation(out=flat[:, 3 * HID : 5 * HID], in_=z_banks[2][:], func=ACT.Sigmoid)
+            return gates, g_hat
 
-            res = work.tile([P, 4, HID], F32)
+        def products(r, gates, g_hat):
+            m = mask_f[:, r : r + 1]
             keep_part = work.tile([P, HID], F32)
             new_part = work.tile([P, HID], F32)
             nc.vector.scalar_tensor_tensor(
@@ -216,25 +245,65 @@ def tile_share_lstm_cell_kernel(
             nc.vector.scalar_tensor_tensor(
                 out=new_part[:], in0=gates[:, 0, :], scalar=m, in1=g_hat[:], op0=ALU.mult, op1=ALU.mult
             )
+            return keep_part, new_part
+
+        def cell_state(r, keep_part, new_part):
+            res = work.tile([P, 4, HID], F32)
             nc.vector.tensor_tensor(out=res[:, 0, :], in0=keep_part[:], in1=new_part[:], op=ALU.add)
+            nc.sync.dma_start(out=out_rows[0][:, r, :], in_=res[:, 0, :])
+            return res
+
+        def tanh_state(res):
             tanh_c = work.tile([P, HID], F32)
             nc.scalar.activation(out=tanh_c[:], in_=res[:, 0, :], func=ACT.Tanh)
+            return tanh_c
+
+        def outputs(r, gates, res, tanh_c):
             nc.vector.scalar_tensor_tensor(
                 out=res[:, 1:4, :],
                 in0=gates[:, 2:5, :],
-                scalar=m,
+                scalar=mask_f[:, r : r + 1],
                 in1=tanh_c[:].unsqueeze(1).to_broadcast([P, 3, HID]),
                 op0=ALU.mult,
                 op1=ALU.mult,
             )
-            for k in range(4):
+            for k in range(1, 4):
                 nc.sync.dma_start(out=out_rows[k][:, r, :], in_=res[:, k, :])
 
-        prepare_rows(0)
-        for j in range(N_CHUNKS):
-            prepare_chunk(j)
-        for r in range(0, HALF):
-            cell(r)
-        prepare_rows(HALF)
-        for r in range(HALF, ROW_TILES):
-            cell(r)
+        out_rows = [o.rearrange("(p r) c -> p r c", r=ROW_TILES) for o in (out_1, out_0, out_2, out_3)]
+
+        transpose_bias()
+        transpose_x(0)
+        transpose_x(1)
+        transpose_weights(0)
+        quantise_x(0)
+        quantise_x(1)
+        mx_transposed(0)
+        transpose_state(0)
+        transpose_weights(1)
+        transpose_weights(2)
+        transpose_state(1)
+        nc.vector.tensor_copy(out=mask_f[:], in_=mask_bf[:])
+        last = None
+        for r in range(ROW_TILES):
+            z_banks = arguments(r)
+            if r == MULTIPLY_AFTER:
+                mx_transposed(1)
+            if last is not None:
+                tanh_c = tanh_state(last[1])
+            gates, g_hat = functions(z_banks)
+            keep_part, new_part = products(r, gates, g_hat)
+            if last is not None:
+                outputs(r - 1, last[0], last[1], tanh_c)
+            if r == PREPARE_AFTER:
+                transpose_x(2)
+                transpose_x(3)
+                transpose_state(2)
+                transpose_state(3)
+            res = cell_state(r, keep_part, new_part)
+            if r == PREPARE_AFTER:
+                quantise_x(2)
+                quantise_x(3)
+            last = (gates, res)
+        tanh_c = tanh_state(last[1])
+        outputs(ROW_TILES - 1, last[0], last[1], tanh_c)

@@ -235,8 +235,9 @@ def tile_share_lstm_cell_kernel(
             nc.scalar.activation(out=flat[:, 3 * HID : 5 * HID], in_=z_banks[2][:], func=ACT.Sigmoid)
             return gates, g_hat
 
-        def products(r, gates, g_hat):
+        def cell_state(r, gates, g_hat):
             m = mask_f[:, r : r + 1]
+            res = work.tile([P, 4, HID], F32)
             keep_part = work.tile([P, HID], F32)
             new_part = work.tile([P, HID], F32)
             nc.vector.scalar_tensor_tensor(
@@ -245,10 +246,6 @@ def tile_share_lstm_cell_kernel(
             nc.vector.scalar_tensor_tensor(
                 out=new_part[:], in0=gates[:, 0, :], scalar=m, in1=g_hat[:], op0=ALU.mult, op1=ALU.mult
             )
-            return keep_part, new_part
-
-        def cell_state(r, keep_part, new_part):
-            res = work.tile([P, 4, HID], F32)
             nc.vector.tensor_tensor(out=res[:, 0, :], in0=keep_part[:], in1=new_part[:], op=ALU.add)
             nc.sync.dma_start(out=out_rows[0][:, r, :], in_=res[:, 0, :])
             return res
@@ -272,12 +269,12 @@ def tile_share_lstm_cell_kernel(
 
         out_rows = [o.rearrange("(p r) c -> p r c", r=ROW_TILES) for o in (out_1, out_0, out_2, out_3)]
 
-        transpose_bias()
         transpose_x(0)
         transpose_x(1)
-        transpose_weights(0)
+        transpose_bias()
         quantise_x(0)
         quantise_x(1)
+        transpose_weights(0)
         mx_transposed(0)
         transpose_state(0)
         transpose_weights(1)
@@ -289,10 +286,10 @@ def tile_share_lstm_cell_kernel(
             z_banks = arguments(r)
             if r == MULTIPLY_AFTER:
                 mx_transposed(1)
+            gates, g_hat = functions(z_banks)
             if last is not None:
                 tanh_c = tanh_state(last[1])
-            gates, g_hat = functions(z_banks)
-            keep_part, new_part = products(r, gates, g_hat)
+            res = cell_state(r, gates, g_hat)
             if last is not None:
                 outputs(r - 1, last[0], last[1], tanh_c)
             if r == PREPARE_AFTER:
@@ -300,8 +297,6 @@ def tile_share_lstm_cell_kernel(
                 transpose_x(3)
                 transpose_state(2)
                 transpose_state(3)
-            res = cell_state(r, keep_part, new_part)
-            if r == PREPARE_AFTER:
                 quantise_x(2)
                 quantise_x(3)
             last = (gates, res)

@@ -21,8 +21,9 @@ CHUNK = 512
 N_CHUNKS = GATES // CHUNK
 PER_BANK = CHUNK // P
 HALF = CHUNK // P
+UNITS = ROW_TILES * N_CHUNKS
 PREPARE_AFTER = 0
-MULTIPLY_AFTER = 2
+MULTIPLY_AFTER = 1
 
 FLOPS = 2 * BATCH * (D_IN * GATES + HID * 4 * HID + HID * 2 * HID)
 
@@ -201,39 +202,26 @@ def tile_share_lstm_cell_kernel(
                         out=mxT[:, half, g, :], in_=mx_bank[:], func=ACT.Identity, bias=bias_col[:, g : g + 1]
                     )
 
-        def arguments(r):
-            z_banks = []
-            for j in range(N_CHUNKS):
-                z_bank = banks.tile([P, CHUNK], F32, tag="bank")
-                for e in range(2):
-                    nc.tensor.matmul(
-                        out=z_bank[:],
-                        lhsT=stateT_bf[:, j // 2, r, e : 2 * P : 2],
-                        rhs=recT_bf[:, 2 * j * CHUNK + e : 2 * (j + 1) * CHUNK : 2],
-                        start=(e == 0),
-                        stop=False,
-                    )
-                for t in range(PER_BANK):
-                    nc.tensor.matmul(
-                        out=z_bank[:, t * P : (t + 1) * P],
-                        lhsT=mxT[:, r // HALF, PER_BANK * j + t, (r % HALF) * P : (r % HALF + 1) * P],
-                        rhs=ident[:],
-                        is_transpose=True,
-                        start=False,
-                        stop=(t == PER_BANK - 1),
-                    )
-                z_banks.append(z_bank)
-            return z_banks
+        def plain_pass(k, e, z_bank):
+            r, j = divmod(k, N_CHUNKS)
+            nc.tensor.matmul(
+                out=z_bank[:],
+                lhsT=stateT_bf[:, j // 2, r, e : 2 * P : 2],
+                rhs=recT_bf[:, 2 * j * CHUNK + e : 2 * (j + 1) * CHUNK : 2],
+                start=(e == 0),
+                stop=False,
+            )
 
-        def functions(z_banks):
-            gates = work.tile([P, 5, HID], F32)
-            g_hat = work.tile([P, HID], F32)
-            flat = gates[:].rearrange("p g c -> p (g c)")
-            nc.scalar.activation(out=flat[:, 0 : 2 * HID], in_=z_banks[0][:], func=ACT.Sigmoid)
-            nc.scalar.activation(out=g_hat[:], in_=z_banks[1][:, HID : 2 * HID], func=ACT.Tanh)
-            nc.scalar.activation(out=flat[:, 2 * HID : 3 * HID], in_=z_banks[1][:, 0:HID], func=ACT.Sigmoid)
-            nc.scalar.activation(out=flat[:, 3 * HID : 5 * HID], in_=z_banks[2][:], func=ACT.Sigmoid)
-            return gates, g_hat
+        def add_back(k, t, z_bank):
+            r, j = divmod(k, N_CHUNKS)
+            nc.tensor.matmul(
+                out=z_bank[:, t * P : (t + 1) * P],
+                lhsT=mxT[:, r // HALF, PER_BANK * j + t, (r % HALF) * P : (r % HALF + 1) * P],
+                rhs=ident[:],
+                is_transpose=True,
+                start=False,
+                stop=(t == PER_BANK - 1),
+            )
 
         def cell_state(r, gates, g_hat):
             m = mask_f[:, r : r + 1]
@@ -281,24 +269,44 @@ def tile_share_lstm_cell_kernel(
         transpose_weights(2)
         transpose_state(1)
         nc.vector.tensor_copy(out=mask_f[:], in_=mask_bf[:])
-        last = None
-        for r in range(ROW_TILES):
-            z_banks = arguments(r)
-            if r == MULTIPLY_AFTER:
-                mx_transposed(1)
-            gates, g_hat = functions(z_banks)
-            if last is not None:
-                tanh_c = tanh_state(last[1])
-            res = cell_state(r, gates, g_hat)
-            if last is not None:
-                outputs(r - 1, last[0], last[1], tanh_c)
-            if r == PREPARE_AFTER:
-                transpose_x(2)
-                transpose_x(3)
-                transpose_state(2)
-                transpose_state(3)
-                quantise_x(2)
-                quantise_x(3)
-            last = (gates, res)
-        tanh_c = tanh_state(last[1])
-        outputs(ROW_TILES - 1, last[0], last[1], tanh_c)
+        z_banks, gates, g_hat, res = {}, {}, {}, {}
+        for k in range(UNITS + 1):
+            if k < UNITS:
+                z_bank = banks.tile([P, CHUNK], F32, tag="bank")
+                z_banks[k] = z_bank
+            for e in range(2):
+                if k < UNITS:
+                    plain_pass(k, e, z_banks[k])
+                if k > 0:
+                    add_back(k - 1, 2 * e, z_banks[k - 1])
+                    add_back(k - 1, 2 * e + 1, z_banks[k - 1])
+            if k == 0:
+                continue
+            r, j = divmod(k - 1, N_CHUNKS)
+            z = z_banks[k - 1]
+            if j == 0:
+                gates_r = work.tile([P, 5, HID], F32)
+                gates[r] = gates_r
+                nc.scalar.activation(out=gates[r][:, 0:2, :].rearrange("p g c -> p (g c)"), in_=z[:], func=ACT.Sigmoid)
+            if j == 1:
+                g_hat_r = work.tile([P, HID], F32)
+                g_hat[r] = g_hat_r
+                nc.scalar.activation(out=g_hat[r][:], in_=z[:, HID : 2 * HID], func=ACT.Tanh)
+                nc.scalar.activation(out=gates[r][:, 2, :], in_=z[:, 0:HID], func=ACT.Sigmoid)
+                res[r] = cell_state(r, gates[r], g_hat[r])
+                if r > 0:
+                    tanh_c = tanh_state(res[r - 1])
+                    outputs(r - 1, gates[r - 1], res[r - 1], tanh_c)
+            if j == 2:
+                nc.scalar.activation(out=gates[r][:, 3:5, :].rearrange("p g c -> p (g c)"), in_=z[:], func=ACT.Sigmoid)
+                if r == PREPARE_AFTER:
+                    transpose_x(2)
+                    transpose_x(3)
+                    transpose_state(2)
+                    transpose_state(3)
+                    quantise_x(2)
+                    quantise_x(3)
+                if r == MULTIPLY_AFTER:
+                    mx_transposed(1)
+        tanh_c = tanh_state(res[ROW_TILES - 1])
+        outputs(ROW_TILES - 1, gates[ROW_TILES - 1], res[ROW_TILES - 1], tanh_c)

@@ -234,9 +234,11 @@ def tile_share_lstm_cell_kernel(
             nc.vector.scalar_tensor_tensor(
                 out=new_part[:], in0=gates[:, 0, :], scalar=m, in1=g_hat[:], op0=ALU.mult, op1=ALU.mult
             )
+            return res, keep_part, new_part
+
+        def sum_state(r, res, keep_part, new_part):
             nc.vector.tensor_tensor(out=res[:, 0, :], in0=keep_part[:], in1=new_part[:], op=ALU.add)
             nc.sync.dma_start(out=out_rows[0][:, r, :], in_=res[:, 0, :])
-            return res
 
         def tanh_state(res):
             tanh_c = work.tile([P, HID], F32)
@@ -293,10 +295,14 @@ def tile_share_lstm_cell_kernel(
                 g_hat[r] = g_hat_r
                 nc.scalar.activation(out=g_hat[r][:], in_=z[:, HID : 2 * HID], func=ACT.Tanh)
                 nc.scalar.activation(out=gates[r][:, 2, :], in_=z[:, 0:HID], func=ACT.Sigmoid)
-                res[r] = cell_state(r, gates[r], g_hat[r])
+                res[r], keep_part, new_part = cell_state(r, gates[r], g_hat[r])
+                if r == ROW_TILES - 1:
+                    sum_state(r, res[r], keep_part, new_part)
                 if r > 0:
                     tanh_c = tanh_state(res[r - 1])
                     outputs(r - 1, gates[r - 1], res[r - 1], tanh_c)
+                if r < ROW_TILES - 1:
+                    sum_state(r, res[r], keep_part, new_part)
             if j == 2:
                 nc.scalar.activation(out=gates[r][:, 3:5, :].rearrange("p g c -> p (g c)"), in_=z[:], func=ACT.Sigmoid)
                 if r == PREPARE_AFTER:

@@ -22,6 +22,8 @@ N_CHUNKS = GATES // CHUNK
 PER_BANK = CHUNK // P
 HALF = CHUNK // P
 UNITS = ROW_TILES * N_CHUNKS
+WARM_FIRST = 4
+WARM_AGAIN = 3
 PREPARE_AFTER = 0
 MULTIPLY_AFTER = 1
 
@@ -54,6 +56,16 @@ def tile_share_lstm_cell_kernel(
         work = stack.enter_context(tc.tile_pool(name="work", bufs=3))
         banks = stack.enter_context(tc.psum_pool(name="banks", bufs=8))
         stack.enter_context(tc.manual_schedule())
+
+        zeros = keep.tile([P, CHUNK], BF16)
+        nc.gpsimd.memset(zeros[:], 0.0)
+        idle_bank = banks.tile([P, CHUNK], F32, tag="bank")
+
+        def idle_passes(n):
+            for i in range(n):
+                nc.tensor.matmul(out=idle_bank[:], lhsT=zeros[:, 0:P], rhs=zeros[:], start=True, stop=True)
+
+        idle_passes(WARM_FIRST)
 
         bias_rows = keep.tile([P, 2, P], BF16)
         nc.vector.memset(bias_rows[:].bitcast(I32), 0)
@@ -265,6 +277,7 @@ def tile_share_lstm_cell_kernel(
         quantise_x(0)
         quantise_x(1)
         transpose_weights(0)
+        idle_passes(WARM_AGAIN)
         mx_transposed(0)
         transpose_state(0)
         transpose_weights(1)

@@ -257,6 +257,18 @@ def tile_share_lstm_cell_kernel(
             nc.scalar.activation(out=tanh_c[:], in_=res[:, 0, :], func=ACT.Tanh)
             return tanh_c
 
+        def last_outputs(r, gates, res, tanh_c):
+            for k in range(1, 4):
+                nc.vector.scalar_tensor_tensor(
+                    out=res[:, k, :],
+                    in0=gates[:, k + 1, :],
+                    scalar=mask_f[:, r : r + 1],
+                    in1=tanh_c[:],
+                    op0=ALU.mult,
+                    op1=ALU.mult,
+                )
+                nc.sync.dma_start(out=out_rows[k][:, r, :], in_=res[:, k, :])
+
         def outputs(r, gates, res, tanh_c):
             nc.vector.scalar_tensor_tensor(
                 out=res[:, 1:4, :],
@@ -328,4 +340,4 @@ def tile_share_lstm_cell_kernel(
                 if r == MULTIPLY_AFTER:
                     mx_transposed(1)
         tanh_c = tanh_state(res[ROW_TILES - 1])
-        outputs(ROW_TILES - 1, gates[ROW_TILES - 1], res[ROW_TILES - 1], tanh_c)
+        last_outputs(ROW_TILES - 1, gates[ROW_TILES - 1], res[ROW_TILES - 1], tanh_c)

@@ -22,6 +22,8 @@ N_CHUNKS = GATES // CHUNK
 PER_BANK = CHUNK // P
 HALF = CHUNK // P
 UNITS = ROW_TILES * N_CHUNKS
+TILE_ORDER = (0, 1, 2, 3, 6, 7, 4, 5, 8, 9, 10, 11)
+G_TILES = (6, 7)
 WARM_FIRST = 4
 WARM_AGAIN = 3
 PREPARE_AFTER = 0
@@ -143,6 +145,7 @@ def tile_share_lstm_cell_kernel(
         recT_bf = recT[:].bitcast(BF16)
         bias_col = keep.tile([P, GATE_TILES], F32)
         mask_f = keep.tile([P, ROW_TILES], F32)
+        mask_2 = keep.tile([P, ROW_TILES], F32)
         mxT = keep.tile([P, ROW_TILES // HALF, GATE_TILES, CHUNK], F32)
 
         def transpose_bias():
@@ -151,6 +154,14 @@ def tile_share_lstm_cell_kernel(
             bias_bank = banks.tile([P, P], F32, tag="bank")
             nc.tensor.transpose(bias_bank[:], bias_gn[:], ident[:])
             nc.vector.tensor_copy(out=bias_col[:], in_=bias_bank[:, 0:GATE_TILES])
+            first_g, last_g = G_TILES
+            nc.vector.tensor_scalar(
+                out=bias_col[:, first_g : last_g + 1],
+                in0=bias_bank[:, first_g : last_g + 1],
+                scalar1=2.0,
+                scalar2=None,
+                op0=ALU.mult,
+            )
 
         def transpose_x(q):
             x_bank = banks.tile([P, PER_BANK, P], F32, tag="bank")
@@ -189,9 +200,20 @@ def tile_share_lstm_cell_kernel(
             rec_bank = banks.tile([P, PER_BANK, P], F32, tag="bank")
             for t in range(PER_BANK):
                 nc.tensor.transpose(rec_bank[:, t, :], rec_words[:, PER_BANK * j + t, :], ident[:])
-            nc.scalar.copy(
-                out=recT[:, j * CHUNK : (j + 1) * CHUNK], in_=rec_bank[:].rearrange("p t n -> p (t n)")
-            )
+            if j != 1:
+                nc.scalar.copy(
+                    out=recT[:, j * CHUNK : (j + 1) * CHUNK], in_=rec_bank[:].rearrange("p t n -> p (t n)")
+                )
+            else:
+                nc.scalar.activation(
+                    out=recT_bf[:, 2 * CHUNK : 3 * CHUNK],
+                    in_=rec_bank[:, 2:4, :].rearrange("p t n -> p (t n)").bitcast(BF16),
+                    func=ACT.Copy,
+                    scale=2.0,
+                )
+                nc.scalar.copy(
+                    out=recT[:, CHUNK + 2 * P : 2 * CHUNK], in_=rec_bank[:, 0:2, :].rearrange("p t n -> p (t n)")
+                )
 
         def mx_transposed(half):
             rows = slice(half * CHUNK, (half + 1) * CHUNK)
@@ -207,11 +229,19 @@ def tile_share_lstm_cell_kernel(
                     start=True,
                     stop=True,
                 )
+                factor = 2.0 if g in G_TILES else 1.0
                 if g % 2 == 0:
-                    nc.vector.tensor_scalar_add(out=mxT[:, half, g, :], in0=mx_bank[:], scalar1=bias_col[:, g : g + 1])
+                    nc.vector.tensor_scalar(
+                        out=mxT[:, half, g, :],
+                        in0=mx_bank[:],
+                        scalar1=factor,
+                        scalar2=bias_col[:, g : g + 1],
+                        op0=ALU.mult,
+                        op1=ALU.add,
+                    )
                 else:
                     nc.scalar.activation(
-                        out=mxT[:, half, g, :], in_=mx_bank[:], func=ACT.Identity, bias=bias_col[:, g : g + 1]
+                        out=mxT[:, half, g, :], in_=mx_bank[:], func=ACT.Identity, bias=bias_col[:, g : g + 1], scale=factor
                     )
 
         def plain_pass(k, e, z_bank):
@@ -228,14 +258,14 @@ def tile_share_lstm_cell_kernel(
             r, j = divmod(k, N_CHUNKS)
             nc.tensor.matmul(
                 out=z_bank[:, t * P : (t + 1) * P],
-                lhsT=mxT[:, r // HALF, PER_BANK * j + t, (r % HALF) * P : (r % HALF + 1) * P],
+                lhsT=mxT[:, r // HALF, TILE_ORDER[PER_BANK * j + t], (r % HALF) * P : (r % HALF + 1) * P],
                 rhs=ident[:],
                 is_transpose=True,
                 start=False,
                 stop=(t == PER_BANK - 1),
             )
 
-        def cell_state(r, gates, g_hat):
+        def cell_state(r, gates):
             m = mask_f[:, r : r + 1]
             res = work.tile([P, 4, HID], F32)
             keep_part = work.tile([P, HID], F32)
@@ -244,12 +274,14 @@ def tile_share_lstm_cell_kernel(
                 out=keep_part[:], in0=gates[:, 1, :], scalar=m, in1=c_sb[:, r, :], op0=ALU.mult, op1=ALU.mult
             )
             nc.vector.scalar_tensor_tensor(
-                out=new_part[:], in0=gates[:, 0, :], scalar=m, in1=g_hat[:], op0=ALU.mult, op1=ALU.mult
+                out=new_part[:], in0=gates[:, 2, :], scalar=-0.5, in1=gates[:, 0, :], op0=ALU.add, op1=ALU.mult
             )
             return res, keep_part, new_part
 
         def sum_state(r, res, keep_part, new_part):
-            nc.vector.tensor_tensor(out=res[:, 0, :], in0=keep_part[:], in1=new_part[:], op=ALU.add)
+            nc.vector.scalar_tensor_tensor(
+                out=res[:, 0, :], in0=new_part[:], scalar=mask_2[:, r : r + 1], in1=keep_part[:], op0=ALU.mult, op1=ALU.add
+            )
             nc.sync.dma_start(out=out_rows[0][:, r, :], in_=res[:, 0, :])
 
         def tanh_state(res):
@@ -261,7 +293,7 @@ def tile_share_lstm_cell_kernel(
             for k in range(1, 4):
                 nc.vector.scalar_tensor_tensor(
                     out=res[:, k, :],
-                    in0=gates[:, k + 1, :],
+                    in0=gates[:, k + 2, :],
                     scalar=mask_f[:, r : r + 1],
                     in1=tanh_c[:],
                     op0=ALU.mult,
@@ -272,7 +304,7 @@ def tile_share_lstm_cell_kernel(
         def outputs(r, gates, res, tanh_c):
             nc.vector.scalar_tensor_tensor(
                 out=res[:, 1:4, :],
-                in0=gates[:, 2:5, :],
+                in0=gates[:, 3:6, :],
                 scalar=mask_f[:, r : r + 1],
                 in1=tanh_c[:].unsqueeze(1).to_broadcast([P, 3, HID]),
                 op0=ALU.mult,
@@ -296,7 +328,8 @@ def tile_share_lstm_cell_kernel(
         transpose_weights(2)
         transpose_state(1)
         nc.vector.tensor_copy(out=mask_f[:], in_=mask_bf[:])
-        z_banks, gates, g_hat, res = {}, {}, {}, {}
+        nc.vector.tensor_scalar(out=mask_2[:], in0=mask_bf[:], scalar1=2.0, scalar2=None, op0=ALU.mult)
+        z_banks, gates, res = {}, {}, {}
         for k in range(UNITS + 1):
             if k < UNITS:
                 z_bank = banks.tile([P, CHUNK], F32, tag="bank")
@@ -312,15 +345,18 @@ def tile_share_lstm_cell_kernel(
             r, j = divmod(k - 1, N_CHUNKS)
             z = z_banks[k - 1]
             if j == 0:
-                gates_r = work.tile([P, 5, HID], F32)
+                gates_r = work.tile([P, 6, HID], F32)
                 gates[r] = gates_r
                 nc.scalar.activation(out=gates[r][:, 0:2, :].rearrange("p g c -> p (g c)"), in_=z[:], func=ACT.Sigmoid)
             if j == 1:
-                g_hat_r = work.tile([P, HID], F32)
-                g_hat[r] = g_hat_r
-                nc.scalar.activation(out=g_hat[r][:], in_=z[:, HID : 2 * HID], func=ACT.Tanh)
-                nc.scalar.activation(out=gates[r][:, 2, :], in_=z[:, 0:HID], func=ACT.Sigmoid)
-                res[r], keep_part, new_part = cell_state(r, gates[r], g_hat[r])
+                if r in (0, ROW_TILES - 1):
+                    nc.scalar.activation(out=gates[r][:, 2, :], in_=z[:, 0:HID], func=ACT.Sigmoid)
+                    nc.scalar.activation(out=gates[r][:, 3, :], in_=z[:, HID : 2 * HID], func=ACT.Sigmoid)
+                else:
+                    nc.scalar.activation(
+                        out=gates[r][:, 2:4, :].rearrange("p g c -> p (g c)"), in_=z[:], func=ACT.Sigmoid
+                    )
+                res[r], keep_part, new_part = cell_state(r, gates[r])
                 if r == ROW_TILES - 1:
                     sum_state(r, res[r], keep_part, new_part)
                 if r > 0:
@@ -329,7 +365,7 @@ def tile_share_lstm_cell_kernel(
                 if r < ROW_TILES - 1:
                     sum_state(r, res[r], keep_part, new_part)
             if j == 2:
-                nc.scalar.activation(out=gates[r][:, 3:5, :].rearrange("p g c -> p (g c)"), in_=z[:], func=ACT.Sigmoid)
+                nc.scalar.activation(out=gates[r][:, 4:6, :].rearrange("p g c -> p (g c)"), in_=z[:], func=ACT.Sigmoid)
                 if r == PREPARE_AFTER:
                     transpose_x(2)
                     transpose_x(3)

@@ -22,12 +22,13 @@ N_CHUNKS = GATES // CHUNK
 PER_BANK = CHUNK // P
 HALF = CHUNK // P
 UNITS = ROW_TILES * N_CHUNKS
+LAST = ROW_TILES - 1
 TILE_ORDER = (0, 1, 2, 3, 6, 7, 4, 5, 8, 9, 10, 11)
 G_TILES = (6, 7)
 WARM_FIRST = 4
 WARM_AGAIN = 3
 PREPARE_AFTER = 0
-MULTIPLY_AFTER = 1
+MULTIPLY_AFTER = (1, 2, 3)
 
 FLOPS = 2 * BATCH * (D_IN * GATES + HID * 4 * HID + HID * 2 * HID)
 
@@ -215,9 +216,9 @@ def tile_share_lstm_cell_kernel(
                     out=recT[:, CHUNK + 2 * P : 2 * CHUNK], in_=rec_bank[:, 0:2, :].rearrange("p t n -> p (t n)")
                 )
 
-        def mx_transposed(half):
+        def mx_transposed(half, gate_tiles):
             rows = slice(half * CHUNK, (half + 1) * CHUNK)
-            for g in range(GATE_TILES):
+            for g in gate_tiles:
                 cols = slice(g * P, (g + 1) * P)
                 mx_bank = banks.tile([P, CHUNK], F32, tag="bank")
                 nc.tensor.matmul_mx(
@@ -244,8 +245,8 @@ def tile_share_lstm_cell_kernel(
                         out=mxT[:, half, g, :], in_=mx_bank[:], func=ACT.Identity, bias=bias_col[:, g : g + 1], scale=factor
                     )
 
-        def plain_pass(k, e, z_bank):
-            r, j = divmod(k, N_CHUNKS)
+        def plain_pass(unit, e, z_bank):
+            r, j = unit
             nc.tensor.matmul(
                 out=z_bank[:],
                 lhsT=stateT_bf[:, j // 2, r, e : 2 * P : 2],
@@ -254,8 +255,8 @@ def tile_share_lstm_cell_kernel(
                 stop=False,
             )
 
-        def add_back(k, t, z_bank):
-            r, j = divmod(k, N_CHUNKS)
+        def add_back(unit, t, z_bank):
+            r, j = unit
             nc.tensor.matmul(
                 out=z_bank[:, t * P : (t + 1) * P],
                 lhsT=mxT[:, r // HALF, TILE_ORDER[PER_BANK * j + t], (r % HALF) * P : (r % HALF + 1) * P],
@@ -289,28 +290,17 @@ def tile_share_lstm_cell_kernel(
             nc.scalar.activation(out=tanh_c[:], in_=res[:, 0, :], func=ACT.Tanh)
             return tanh_c
 
-        def last_outputs(r, gates, res, tanh_c):
-            for k in range(1, 4):
-                nc.vector.scalar_tensor_tensor(
-                    out=res[:, k, :],
-                    in0=gates[:, k + 2, :],
-                    scalar=mask_f[:, r : r + 1],
-                    in1=tanh_c[:],
-                    op0=ALU.mult,
-                    op1=ALU.mult,
-                )
-                nc.sync.dma_start(out=out_rows[k][:, r, :], in_=res[:, k, :])
-
-        def outputs(r, gates, res, tanh_c):
+        def outputs(r, gates, res, tanh_c, first, last):
+            n = last - first + 1
             nc.vector.scalar_tensor_tensor(
-                out=res[:, 1:4, :],
-                in0=gates[:, 3:6, :],
+                out=res[:, first : last + 1, :],
+                in0=gates[:, first + 2 : last + 3, :],
                 scalar=mask_f[:, r : r + 1],
-                in1=tanh_c[:].unsqueeze(1).to_broadcast([P, 3, HID]),
+                in1=tanh_c[:].unsqueeze(1).to_broadcast([P, n, HID]),
                 op0=ALU.mult,
                 op1=ALU.mult,
             )
-            for k in range(1, 4):
+            for k in range(first, last + 1):
                 nc.sync.dma_start(out=out_rows[k][:, r, :], in_=res[:, k, :])
 
         out_rows = [o.rearrange("(p r) c -> p r c", r=ROW_TILES) for o in (out_1, out_0, out_2, out_3)]
@@ -322,34 +312,37 @@ def tile_share_lstm_cell_kernel(
         quantise_x(1)
         transpose_weights(0)
         idle_passes(WARM_AGAIN)
-        mx_transposed(0)
+        mx_transposed(0, range(GATE_TILES))
         transpose_state(0)
         transpose_weights(1)
         transpose_weights(2)
         transpose_state(1)
         nc.vector.tensor_copy(out=mask_f[:], in_=mask_bf[:])
         nc.vector.tensor_scalar(out=mask_2[:], in0=mask_bf[:], scalar1=2.0, scalar2=None, op0=ALU.mult)
-        z_banks, gates, res = {}, {}, {}
+        units = [divmod(k, N_CHUNKS) for k in range(UNITS)]
+        units.remove((LAST - 1, 2))
+        units.insert(-1, (LAST - 1, 2))
+        z_banks, gates, res, tanh = {}, {}, {}, {}
         for k in range(UNITS + 1):
             if k < UNITS:
                 z_bank = banks.tile([P, CHUNK], F32, tag="bank")
                 z_banks[k] = z_bank
             for e in range(2):
                 if k < UNITS:
-                    plain_pass(k, e, z_banks[k])
+                    plain_pass(units[k], e, z_banks[k])
                 if k > 0:
-                    add_back(k - 1, 2 * e, z_banks[k - 1])
-                    add_back(k - 1, 2 * e + 1, z_banks[k - 1])
+                    add_back(units[k - 1], 2 * e, z_banks[k - 1])
+                    add_back(units[k - 1], 2 * e + 1, z_banks[k - 1])
             if k == 0:
                 continue
-            r, j = divmod(k - 1, N_CHUNKS)
+            r, j = units[k - 1]
             z = z_banks[k - 1]
             if j == 0:
                 gates_r = work.tile([P, 6, HID], F32)
                 gates[r] = gates_r
                 nc.scalar.activation(out=gates[r][:, 0:2, :].rearrange("p g c -> p (g c)"), in_=z[:], func=ACT.Sigmoid)
             if j == 1:
-                if r in (0, ROW_TILES - 1):
+                if r in (0, LAST):
                     nc.scalar.activation(out=gates[r][:, 2, :], in_=z[:, 0:HID], func=ACT.Sigmoid)
                     nc.scalar.activation(out=gates[r][:, 3, :], in_=z[:, HID : 2 * HID], func=ACT.Sigmoid)
                 else:
@@ -357,15 +350,23 @@ def tile_share_lstm_cell_kernel(
                         out=gates[r][:, 2:4, :].rearrange("p g c -> p (g c)"), in_=z[:], func=ACT.Sigmoid
                     )
                 res[r], keep_part, new_part = cell_state(r, gates[r])
-                if r == ROW_TILES - 1:
+                if r == LAST:
                     sum_state(r, res[r], keep_part, new_part)
                 if r > 0:
-                    tanh_c = tanh_state(res[r - 1])
-                    outputs(r - 1, gates[r - 1], res[r - 1], tanh_c)
-                if r < ROW_TILES - 1:
+                    tanh[r - 1] = tanh_state(res[r - 1])
+                    outputs(r - 1, gates[r - 1], res[r - 1], tanh[r - 1], 1, 1 if r == LAST else 3)
+                if r < LAST:
                     sum_state(r, res[r], keep_part, new_part)
-            if j == 2:
+            if j == 2 and r == LAST:
+                for g in range(2):
+                    nc.scalar.activation(out=gates[r][:, 4 + g, :], in_=z[:, g * HID : (g + 1) * HID], func=ACT.Sigmoid)
+                    outputs(r, gates[r], res[r], tanh[r], 2 + g, 2 + g)
+            if j == 2 and r < LAST:
                 nc.scalar.activation(out=gates[r][:, 4:6, :].rearrange("p g c -> p (g c)"), in_=z[:], func=ACT.Sigmoid)
+                if r == LAST - 1:
+                    outputs(r, gates[r], res[r], tanh[r], 2, 3)
+                    tanh[LAST] = tanh_state(res[LAST])
+                    outputs(LAST, gates[LAST], res[LAST], tanh[LAST], 1, 1)
                 if r == PREPARE_AFTER:
                     transpose_x(2)
                     transpose_x(3)
@@ -373,7 +374,6 @@ def tile_share_lstm_cell_kernel(
                     transpose_state(3)
                     quantise_x(2)
                     quantise_x(3)
-                if r == MULTIPLY_AFTER:
-                    mx_transposed(1)
-        tanh_c = tanh_state(res[ROW_TILES - 1])
-        last_outputs(ROW_TILES - 1, gates[ROW_TILES - 1], res[ROW_TILES - 1], tanh_c)
+                if r in MULTIPLY_AFTER:
+                    i = MULTIPLY_AFTER.index(r)
+                    mx_transposed(1, range(i * PER_BANK, (i + 1) * PER_BANK))

@@ -27,8 +27,6 @@ TILE_ORDER = (0, 1, 2, 3, 6, 7, 4, 5, 8, 9, 10, 11)
 G_TILES = (6, 7)
 WARM_FIRST = 4
 WARM_AGAIN = 3
-PREPARE_AFTER = 0
-MULTIPLY_AFTER = (1, 2, 3)
 
 FLOPS = 2 * BATCH * (D_IN * GATES + HID * 4 * HID + HID * 2 * HID)
 
@@ -61,7 +59,7 @@ def tile_share_lstm_cell_kernel(
         stack.enter_context(tc.manual_schedule())
 
         zeros = keep.tile([P, CHUNK], BF16)
-        nc.gpsimd.memset(zeros[:], 0.0)
+        nc.vector.memset(zeros[:].bitcast(I32), 0)
         idle_bank = banks.tile([P, CHUNK], F32, tag="bank")
 
         def idle_passes(n):
@@ -111,24 +109,24 @@ def tile_share_lstm_cell_kernel(
             cols = slice(j * CHUNK, (j + 1) * CHUNK)
             nc.sync.dma_start(out=w_words[:, cols].bitcast(I32), in_=words_i32[:, cols])
 
+        nc.gpsimd.dma_start(out=rec_sb[:, 0:4, :], in_=hh_rows[:, 0:4, :])
         nc.gpsimd.dma_start(out=mask_bf[:], in_=mask.rearrange("(p r) -> p r", r=ROW_TILES))
         load_x(0)
         load_x(1)
-        nc.sync.dma_start(out=rec_sb[:, 0:4, :], in_=hh_rows[:, 0:4, :])
+        load_w_words(0)
         for quad in range(4):
             nc.sync.dma_start(
                 out=w_plane[32 * quad : 32 * quad + 4, :].bitcast(I32),
                 in_=scales_i32[4 * quad : 4 * quad + 4, :],
             )
-        load_w_words(0)
         load_w_words(1)
         load_w_words(2)
         load_state(0)
         nc.sync.dma_start(out=rec_sb[:, 4:8, :], in_=hh_rows[:, 4:8, :])
         nc.sync.dma_start(out=rec_sb[:, 8:12, :], in_=sh_rows)
-        load_state(1)
-        nc.sync.dma_start(out=c_sb[:], in_=c_minors.rearrange("(p r) k -> p r k", r=ROW_TILES))
         load_x(2)
+        nc.sync.dma_start(out=c_sb[:], in_=c_minors.rearrange("(p r) k -> p r k", r=ROW_TILES))
+        load_state(1)
         load_x(3)
         load_state(2)
         load_state(3)
@@ -149,9 +147,12 @@ def tile_share_lstm_cell_kernel(
         mask_2 = keep.tile([P, ROW_TILES], F32)
         mxT = keep.tile([P, ROW_TILES // HALF, GATE_TILES, CHUNK], F32)
 
-        def transpose_bias():
-            bias_gn = keep.tile([P, P], F32)
+        bias_gn = keep.tile([P, P], F32)
+
+        def add_biases():
             nc.vector.tensor_tensor(out=bias_gn[:], in0=bias_rows[:, 0, :], in1=bias_rows[:, 1, :], op=ALU.add)
+
+        def transpose_bias():
             bias_bank = banks.tile([P, P], F32, tag="bank")
             nc.tensor.transpose(bias_bank[:], bias_gn[:], ident[:])
             nc.vector.tensor_copy(out=bias_col[:], in_=bias_bank[:, 0:GATE_TILES])
@@ -202,9 +203,8 @@ def tile_share_lstm_cell_kernel(
             for t in range(PER_BANK):
                 nc.tensor.transpose(rec_bank[:, t, :], rec_words[:, PER_BANK * j + t, :], ident[:])
             if j != 1:
-                nc.scalar.copy(
-                    out=recT[:, j * CHUNK : (j + 1) * CHUNK], in_=rec_bank[:].rearrange("p t n -> p (t n)")
-                )
+                copy = nc.scalar.copy if j == 0 else nc.vector.tensor_copy
+                copy(out=recT[:, j * CHUNK : (j + 1) * CHUNK], in_=rec_bank[:].rearrange("p t n -> p (t n)"))
             else:
                 nc.scalar.activation(
                     out=recT_bf[:, 2 * CHUNK : 3 * CHUNK],
@@ -244,6 +244,9 @@ def tile_share_lstm_cell_kernel(
                     nc.scalar.activation(
                         out=mxT[:, half, g, :], in_=mx_bank[:], func=ACT.Identity, bias=bias_col[:, g : g + 1], scale=factor
                     )
+
+        def mx_second(i):
+            mx_transposed(1, range(2 * i, 2 * i + 2))
 
         def plain_pass(unit, e, z_bank):
             r, j = unit
@@ -306,22 +309,33 @@ def tile_share_lstm_cell_kernel(
         out_rows = [o.rearrange("(p r) c -> p r c", r=ROW_TILES) for o in (out_1, out_0, out_2, out_3)]
 
         transpose_x(0)
+        add_biases()
         transpose_x(1)
-        transpose_bias()
         quantise_x(0)
         quantise_x(1)
-        transpose_weights(0)
         idle_passes(WARM_AGAIN)
-        mx_transposed(0, range(GATE_TILES))
+        transpose_bias()
+        transpose_weights(0)
+        mx_transposed(0, range(0, 2 * PER_BANK))
         transpose_state(0)
+        mx_transposed(0, range(2 * PER_BANK, GATE_TILES))
         transpose_weights(1)
         transpose_weights(2)
-        transpose_state(1)
         nc.vector.tensor_copy(out=mask_f[:], in_=mask_bf[:])
         nc.vector.tensor_scalar(out=mask_2[:], in0=mask_bf[:], scalar1=2.0, scalar2=None, op0=ALU.mult)
         units = [divmod(k, N_CHUNKS) for k in range(UNITS)]
         units.remove((LAST - 1, 2))
         units.insert(-1, (LAST - 1, 2))
+        behind = {
+            0: [(transpose_x, 2)],
+            2: [(quantise_x, 2)],
+            3: [(transpose_state, 1)],
+            4: [(transpose_x, 3), (quantise_x, 3)],
+            6: [(transpose_state, 2)],
+            12: [(transpose_state, 3)],
+        }
+        for i in range(GATE_TILES // 2):
+            behind.setdefault(N_CHUNKS * 3 - 1 + i, []).append((mx_second, i))
         z_banks, gates, res, tanh = {}, {}, {}, {}
         for k in range(UNITS + 1):
             if k < UNITS:
@@ -330,13 +344,17 @@ def tile_share_lstm_cell_kernel(
             for e in range(2):
                 if k < UNITS:
                     plain_pass(units[k], e, z_banks[k])
-                if k > 0:
+                if k > 1:
                     add_back(units[k - 1], 2 * e, z_banks[k - 1])
                     add_back(units[k - 1], 2 * e + 1, z_banks[k - 1])
             if k == 0:
+                for t in range(PER_BANK):
+                    add_back(units[0], t, z_banks[0])
+            closed = max(k - 1, 0)
+            r, j = units[closed]
+            z = z_banks[closed]
+            if k == 1:
                 continue
-            r, j = units[k - 1]
-            z = z_banks[k - 1]
             if j == 0:
                 gates_r = work.tile([P, 6, HID], F32)
                 gates[r] = gates_r
@@ -367,13 +385,5 @@ def tile_share_lstm_cell_kernel(
                     outputs(r, gates[r], res[r], tanh[r], 2, 3)
                     tanh[LAST] = tanh_state(res[LAST])
                     outputs(LAST, gates[LAST], res[LAST], tanh[LAST], 1, 1)
-                if r == PREPARE_AFTER:
-                    transpose_x(2)
-                    transpose_x(3)
-                    transpose_state(2)
-                    transpose_state(3)
-                    quantise_x(2)
-                    quantise_x(3)
-                if r in MULTIPLY_AFTER:
-                    i = MULTIPLY_AFTER.index(r)
-                    mx_transposed(1, range(i * PER_BANK, (i + 1) * PER_BANK))
+            for job, which in behind.get(k, ()):
+                job(which)

@@ -216,37 +216,47 @@ def tile_share_lstm_cell_kernel(
                     out=recT[:, CHUNK + 2 * P : 2 * CHUNK], in_=rec_bank[:, 0:2, :].rearrange("p t n -> p (t n)")
                 )
 
-        def mx_transposed(half, gate_tiles):
-            rows = slice(half * CHUNK, (half + 1) * CHUNK)
-            for g in gate_tiles:
-                cols = slice(g * P, (g + 1) * P)
-                mx_bank = banks.tile([P, CHUNK], F32, tag="bank")
-                nc.tensor.matmul_mx(
-                    out=mx_bank[:],
-                    lhsT=w_words[:, cols].bitcast(FP8X4),
-                    lhsT_scale=w_plane[:, cols],
-                    rhs=x_codes[:, rows].bitcast(FP8X4),
-                    rhs_scale=x_plane[:, rows],
-                    start=True,
-                    stop=True,
-                )
-                factor = 2.0 if g in G_TILES else 1.0
-                if g % 2 == 0:
-                    nc.vector.tensor_scalar(
-                        out=mxT[:, half, g, :],
-                        in0=mx_bank[:],
-                        scalar1=factor,
-                        scalar2=bias_col[:, g : g + 1],
-                        op0=ALU.mult,
-                        op1=ALU.add,
-                    )
-                else:
-                    nc.scalar.activation(
-                        out=mxT[:, half, g, :], in_=mx_bank[:], func=ACT.Identity, bias=bias_col[:, g : g + 1], scale=factor
-                    )
+        mx_banks = {}
 
-        def mx_second(i):
-            mx_transposed(1, range(2 * i, 2 * i + 2))
+        def mx_pass(half, g):
+            rows = slice(half * CHUNK, (half + 1) * CHUNK)
+            cols = slice(g * P, (g + 1) * P)
+            mx_bank = banks.tile([P, CHUNK], F32, tag="bank")
+            mx_banks[g] = mx_bank
+            nc.tensor.matmul_mx(
+                out=mx_bank[:],
+                lhsT=w_words[:, cols].bitcast(FP8X4),
+                lhsT_scale=w_plane[:, cols],
+                rhs=x_codes[:, rows].bitcast(FP8X4),
+                rhs_scale=x_plane[:, rows],
+                start=True,
+                stop=True,
+            )
+
+        def mx_leave(half, g):
+            factor = 2.0 if g in G_TILES else 1.0
+            if g % 2 == 0:
+                nc.vector.tensor_scalar(
+                    out=mxT[:, half, g, :],
+                    in0=mx_banks[g][:],
+                    scalar1=factor,
+                    scalar2=bias_col[:, g : g + 1],
+                    op0=ALU.mult,
+                    op1=ALU.add,
+                )
+            else:
+                nc.scalar.activation(
+                    out=mxT[:, half, g, :],
+                    in_=mx_banks[g][:],
+                    func=ACT.Identity,
+                    bias=bias_col[:, g : g + 1],
+                    scale=factor,
+                )
+
+        def mx_transposed(half, gate_tiles):
+            for g in gate_tiles:
+                mx_pass(half, g)
+                mx_leave(half, g)
 
         def plain_pass(unit, e, z_bank):
             r, j = unit
@@ -318,8 +328,8 @@ def tile_share_lstm_cell_kernel(
         transpose_weights(0)
         mx_transposed(0, range(0, 2 * PER_BANK))
         transpose_state(0)
-        mx_transposed(0, range(2 * PER_BANK, GATE_TILES))
         transpose_weights(1)
+        mx_transposed(0, range(2 * PER_BANK, GATE_TILES))
         transpose_weights(2)
         nc.vector.tensor_copy(out=mask_f[:], in_=mask_bf[:])
         nc.vector.tensor_scalar(out=mask_2[:], in0=mask_bf[:], scalar1=2.0, scalar2=None, op0=ALU.mult)
@@ -327,15 +337,13 @@ def tile_share_lstm_cell_kernel(
         units.remove((LAST - 1, 2))
         units.insert(-1, (LAST - 1, 2))
         behind = {
-            0: [(transpose_x, 2)],
-            2: [(quantise_x, 2)],
+            2: [(transpose_x, 2)],
             3: [(transpose_state, 1)],
-            4: [(transpose_x, 3), (quantise_x, 3)],
+            4: [(transpose_x, 3), (quantise_x, 2), (quantise_x, 3)],
             6: [(transpose_state, 2)],
             12: [(transpose_state, 3)],
         }
-        for i in range(GATE_TILES // 2):
-            behind.setdefault(N_CHUNKS * 3 - 1 + i, []).append((mx_second, i))
+        pairs = {N_CHUNKS * 3 - 1 + i: i for i in range(GATE_TILES // 2)}
         z_banks, gates, res, tanh = {}, {}, {}, {}
         for k in range(UNITS + 1):
             if k < UNITS:
@@ -344,17 +352,17 @@ def tile_share_lstm_cell_kernel(
             for e in range(2):
                 if k < UNITS:
                     plain_pass(units[k], e, z_banks[k])
-                if k > 1:
+                if k > 0:
                     add_back(units[k - 1], 2 * e, z_banks[k - 1])
                     add_back(units[k - 1], 2 * e + 1, z_banks[k - 1])
             if k == 0:
-                for t in range(PER_BANK):
-                    add_back(units[0], t, z_banks[0])
-            closed = max(k - 1, 0)
-            r, j = units[closed]
-            z = z_banks[closed]
-            if k == 1:
                 continue
+            if k in pairs:
+                for g in range(2):
+                    mx_pass(1, 2 * pairs[k] + g)
+                mx_leave(1, 2 * pairs[k])
+            r, j = units[k - 1]
+            z = z_banks[k - 1]
             if j == 0:
                 gates_r = work.tile([P, 6, HID], F32)
                 gates[r] = gates_r
@@ -387,3 +395,5 @@ def tile_share_lstm_cell_kernel(
                     outputs(LAST, gates[LAST], res[LAST], tanh[LAST], 1, 1)
             for job, which in behind.get(k, ()):
                 job(which)
+            if k in pairs:
+                mx_leave(1, 2 * pairs[k] + 1)

@@ -135,6 +135,7 @@ def tile_share_lstm_cell_kernel(
         state_words = state_sb[:].bitcast(F32)
         rec_words = rec_sb[:].bitcast(F32)
 
+        x_apart = keep.tile([P, HALF, 2, P], I32)
         x_grouped = keep.tile([P, ROW_TILES, 4 * P], BF16, align_bytes=64)
         x_codes = keep.tile([P, ROW_TILES * P], U32, align_bytes=64)
         x_plane = keep.tile([P, ROW_TILES * P], U8, align_bytes=64)
@@ -165,13 +166,22 @@ def tile_share_lstm_cell_kernel(
                 op0=ALU.mult,
             )
 
+        def part_x(q):
+            rows = slice(2 * q - HALF, 2 * q - HALF + 2)
+            nc.gpsimd.tensor_copy(
+                out=x_apart[:, rows, :, :],
+                in_=x_sb[:, 2 * q : 2 * q + 2, :].bitcast(I32).rearrange("p r (w u) -> p r u w", u=2),
+            )
+
         def transpose_x(q):
             x_bank = banks.tile([P, PER_BANK, P], F32, tag="bank")
             for r in range(2):
                 for u in range(2):
-                    nc.tensor.transpose(
-                        x_bank[:, 2 * r + u, :], x_words[:, 2 * q + r, u : D_IN // 2 : 2], ident[:]
-                    )
+                    if 2 * q < HALF:
+                        words = x_words[:, 2 * q + r, u : D_IN // 2 : 2]
+                    else:
+                        words = x_apart[:, 2 * q - HALF + r, u, :].bitcast(F32)
+                    nc.tensor.transpose(x_bank[:, 2 * r + u, :], words, ident[:])
             side_by_side = x_grouped[:, 2 * q : 2 * q + 2, :].bitcast(F32).rearrange("p r (b u) -> p r b u", u=2)
             by_word = x_bank[:].rearrange("p (r u) b -> p r b u", u=2)
             if q % 2 == 0:
@@ -318,6 +328,8 @@ def tile_share_lstm_cell_kernel(
 
         out_rows = [o.rearrange("(p r) c -> p r c", r=ROW_TILES) for o in (out_1, out_0, out_2, out_3)]
 
+        part_x(2)
+        part_x(3)
         transpose_x(0)
         add_biases()
         transpose_x(1)

@@ -349,13 +349,14 @@ def tile_share_lstm_cell_kernel(
         units.remove((LAST - 1, 2))
         units.insert(-1, (LAST - 1, 2))
         behind = {
-            2: [(transpose_x, 2)],
-            3: [(transpose_state, 1)],
-            4: [(transpose_x, 3), (quantise_x, 2), (quantise_x, 3)],
+            1: [(transpose_x, 2), (quantise_x, 2)],
+            2: [(transpose_state, 1)],
+            3: [(transpose_x, 3)],
+            4: [(quantise_x, 3)],
             6: [(transpose_state, 2)],
             12: [(transpose_state, 3)],
         }
-        pairs = {N_CHUNKS * 3 - 1 + i: i for i in range(GATE_TILES // 2)}
+        pairs = {N_CHUNKS * 2 + 1 + i: i for i in range(GATE_TILES // 2)}
         z_banks, gates, res, tanh = {}, {}, {}, {}
         for k in range(UNITS + 1):
             if k < UNITS:

@@ -54,7 +54,7 @@ def tile_share_lstm_cell_kernel(
     nc = tc.nc
     with ExitStack() as stack:
         keep = stack.enter_context(tc.tile_pool(name="keep", bufs=1))
-        work = stack.enter_context(tc.tile_pool(name="work", bufs=3))
+        work = stack.enter_context(tc.tile_pool(name="work", bufs=4))
         banks = stack.enter_context(tc.psum_pool(name="banks", bufs=8))
         stack.enter_context(tc.manual_schedule())
 
@@ -346,12 +346,14 @@ def tile_share_lstm_cell_kernel(
         nc.vector.tensor_copy(out=mask_f[:], in_=mask_bf[:])
         nc.vector.tensor_scalar(out=mask_2[:], in0=mask_bf[:], scalar1=2.0, scalar2=None, op0=ALU.mult)
         units = [divmod(k, N_CHUNKS) for k in range(UNITS)]
-        units.remove((LAST - 1, 2))
-        units.insert(-1, (LAST - 1, 2))
+        late = range(LAST - 2, LAST)
+        for r in late:
+            units.remove((r, 2))
+            units.insert(-1, (r, 2))
         behind = {
-            1: [(transpose_x, 2), (quantise_x, 2)],
-            2: [(transpose_state, 1)],
-            3: [(transpose_x, 3)],
+            1: [(transpose_state, 1)],
+            2: [(transpose_x, 2)],
+            3: [(transpose_x, 3), (quantise_x, 2)],
             4: [(quantise_x, 3)],
             6: [(transpose_state, 2)],
             12: [(transpose_state, 3)],
@@ -393,7 +395,7 @@ def tile_share_lstm_cell_kernel(
                     sum_state(r, res[r], keep_part, new_part)
                 if r > 0:
                     tanh[r - 1] = tanh_state(res[r - 1])
-                    outputs(r - 1, gates[r - 1], res[r - 1], tanh[r - 1], 1, 1 if r == LAST else 3)
+                    outputs(r - 1, gates[r - 1], res[r - 1], tanh[r - 1], 1, 1 if r - 1 in late else 3)
                 if r < LAST:
                     sum_state(r, res[r], keep_part, new_part)
             if j == 2 and r == LAST:
@@ -402,8 +404,9 @@ def tile_share_lstm_cell_kernel(
                     outputs(r, gates[r], res[r], tanh[r], 2 + g, 2 + g)
             if j == 2 and r < LAST:
                 nc.scalar.activation(out=gates[r][:, 4:6, :].rearrange("p g c -> p (g c)"), in_=z[:], func=ACT.Sigmoid)
-                if r == LAST - 1:
+                if r in late:
                     outputs(r, gates[r], res[r], tanh[r], 2, 3)
+                if r == late[-1]:
                     tanh[LAST] = tanh_state(res[LAST])
                     outputs(LAST, gates[LAST], res[LAST], tanh[LAST], 1, 1)
             for job, which in behind.get(k, ()):

@@ -70,7 +70,9 @@ def tile_share_lstm_cell_kernel(
 
         bias_rows = keep.tile([P, 2, P], BF16)
         nc.vector.memset(bias_rows[:].bitcast(I32), 0)
-        nc.scalar.dma_start(out=bias_rows[0:GATE_TILES, 0, :], in_=bias_ih.rearrange("(g n) -> g n", n=P))
+        ih_rows = bias_ih.rearrange("(g n) -> g n", n=P)
+        for rows in (slice(0, 8), slice(8, GATE_TILES)):
+            nc.scalar.dma_start(out=bias_rows[rows, 0, :], in_=ih_rows[rows, :])
         nc.scalar.dma_start(out=bias_rows[0:8, 1, :], in_=bias_hh.rearrange("(g n) -> g n", n=P))
         nc.scalar.dma_start(out=bias_rows[8:GATE_TILES, 1, :], in_=bias_sh.rearrange("(g n) -> g n", n=P))
         w_plane = keep.tile([P, GATES], U8, align_bytes=64)

from contextlib import ExitStack

import concourse.mybir as mybir
from concourse.masks import make_identity

F32 = mybir.dt.float32
BF16 = mybir.dt.bfloat16
I32 = mybir.dt.int32
U32 = mybir.dt.uint32
U8 = mybir.dt.uint8
FP8X4 = mybir.dt.float8_e4m3fn_x4
ACT = mybir.ActivationFunctionType
ALU = mybir.AluOpType

P = 128
BATCH, D_IN, HID = 1024, 512, 256
GATES = 6 * HID
GATE_TILES = GATES // P
ROW_TILES = BATCH // P
CHUNK = 512
N_CHUNKS = GATES // CHUNK
PER_BANK = CHUNK // P
HALF = CHUNK // P
UNITS = ROW_TILES * N_CHUNKS
LAST = ROW_TILES - 1
TILE_ORDER = (0, 1, 2, 3, 6, 7, 4, 5, 8, 9, 10, 11)
G_TILES = (6, 7)
WARM_FIRST = 4
WARM_AGAIN = 3

FLOPS = 2 * BATCH * (D_IN * GATES + HID * 4 * HID + HID * 2 * HID)


def tile_share_lstm_cell_kernel(
    tc,
    x,
    h_minors,
    c_minors,
    s_minors,
    mask,
    weight_ih_words,
    weight_ih_scales,
    weight_hh,
    weight_sh,
    bias_ih,
    bias_hh,
    bias_sh,
    idx,
    out_0,
    out_1,
    out_2,
    out_3,
):
    nc = tc.nc
    with ExitStack() as stack:
        keep = stack.enter_context(tc.tile_pool(name="keep", bufs=1))
        work = stack.enter_context(tc.tile_pool(name="work", bufs=4))
        banks = stack.enter_context(tc.psum_pool(name="banks", bufs=8))
        stack.enter_context(tc.manual_schedule())

        zeros = keep.tile([P, CHUNK], BF16)
        nc.vector.memset(zeros[:].bitcast(I32), 0)
        idle_bank = banks.tile([P, CHUNK], F32, tag="bank")

        def idle_passes(n):
            for i in range(n):
                nc.tensor.matmul(out=idle_bank[:], lhsT=zeros[:, 0:P], rhs=zeros[:], start=True, stop=True)

        idle_passes(WARM_FIRST)

        bias_rows = keep.tile([P, 2, P], BF16)
        nc.vector.memset(bias_rows[:].bitcast(I32), 0)
        ih_rows = bias_ih.rearrange("(g n) -> g n", n=P)
        for rows in (slice(0, 8), slice(8, GATE_TILES)):
            nc.scalar.dma_start(out=bias_rows[rows, 0, :], in_=ih_rows[rows, :])
        nc.scalar.dma_start(out=bias_rows[0:8, 1, :], in_=bias_hh.rearrange("(g n) -> g n", n=P))
        nc.scalar.dma_start(out=bias_rows[8:GATE_TILES, 1, :], in_=bias_sh.rearrange("(g n) -> g n", n=P))
        w_plane = keep.tile([P, GATES], U8, align_bytes=64)
        nc.vector.memset(w_plane[:].bitcast(I32), 0)
        warm = keep.tile([P, 1], F32)
        nc.vector.memset(warm[:], 0.0)
        nc.scalar.activation(out=warm[:], in_=warm[:], func=ACT.Sigmoid)
        ident = keep.tile([P, P], F32)
        make_identity(nc, ident[:])

        x_sb = keep.tile([P, ROW_TILES, D_IN], BF16)
        state_sb = keep.tile([P, 2, ROW_TILES, HID], BF16)
        c_sb = keep.tile([P, ROW_TILES, HID], BF16)
        rec_sb = keep.tile([P, GATE_TILES, HID], BF16)
        w_words = keep.tile([P, GATES], U32, align_bytes=64)
        mask_bf = keep.tile([P, ROW_TILES], BF16)

        x_rows = x.rearrange("(p r) k -> p r k", r=ROW_TILES)
        h_rows = h_minors.rearrange("(p r) k -> p r k", r=ROW_TILES)
        s_rows = s_minors[idx].rearrange("(p r) k -> p r k", r=ROW_TILES)
        hh_rows = weight_hh.rearrange("(t p) k -> p t k", p=P)
        sh_rows = weight_sh.rearrange("(t p) k -> p t k", p=P)
        words_i32 = weight_ih_words[0].rearrange("p n t -> p (n t)").bitcast(I32)
        scales_i32 = weight_ih_scales[0].bitcast(I32)

        def load_x(q):
            rows = slice(2 * q, 2 * q + 2)
            nc.sync.dma_start(out=x_sb[:, rows, :], in_=x_rows[:, rows, :])

        def load_state(q):
            rows = slice(2 * q, 2 * q + 2)
            nc.sync.dma_start(out=state_sb[:, 0, rows, :], in_=h_rows[:, rows, :])
            nc.sync.dma_start(out=state_sb[:, 1, rows, :], in_=s_rows[:, rows, :])

        def load_w_words(j):
            cols = slice(j * CHUNK, (j + 1) * CHUNK)
            nc.sync.dma_start(out=w_words[:, cols].bitcast(I32), in_=words_i32[:, cols])

        nc.gpsimd.dma_start(out=rec_sb[:, 0:4, :], in_=hh_rows[:, 0:4, :])
        nc.gpsimd.dma_start(out=mask_bf[:], in_=mask.rearrange("(p r) -> p r", r=ROW_TILES))
        load_x(0)
        load_x(1)
        load_w_words(0)
        for quad in range(4):
            nc.sync.dma_start(
                out=w_plane[32 * quad : 32 * quad + 4, :].bitcast(I32),
                in_=scales_i32[4 * quad : 4 * quad + 4, :],
            )
        load_w_words(1)
        load_w_words(2)
        load_state(0)
        nc.sync.dma_start(out=rec_sb[:, 4:8, :], in_=hh_rows[:, 4:8, :])
        nc.sync.dma_start(out=rec_sb[:, 8:12, :], in_=sh_rows)
        load_x(2)
        nc.sync.dma_start(out=c_sb[:], in_=c_minors.rearrange("(p r) k -> p r k", r=ROW_TILES))
        load_state(1)
        load_x(3)
        load_state(2)
        load_state(3)

        x_words = x_sb[:].bitcast(F32)
        state_words = state_sb[:].bitcast(F32)
        rec_words = rec_sb[:].bitcast(F32)

        x_apart = keep.tile([P, HALF, 2, P], I32)
        x_grouped = keep.tile([P, ROW_TILES, 4 * P], BF16, align_bytes=64)
        x_codes = keep.tile([P, ROW_TILES * P], U32, align_bytes=64)
        x_plane = keep.tile([P, ROW_TILES * P], U8, align_bytes=64)
        stateT = keep.tile([P, 2, ROW_TILES, P], F32)
        recT = keep.tile([P, GATES], F32)
        stateT_bf = stateT[:].bitcast(BF16)
        recT_bf = recT[:].bitcast(BF16)
        bias_col = keep.tile([P, GATE_TILES], F32)
        mask_f = keep.tile([P, ROW_TILES], F32)
        mask_2 = keep.tile([P, ROW_TILES], F32)
        mxT = keep.tile([P, ROW_TILES // HALF, GATE_TILES, CHUNK], F32)

        bias_gn = keep.tile([P, P], F32)

        def add_biases():
            nc.vector.tensor_tensor(out=bias_gn[:], in0=bias_rows[:, 0, :], in1=bias_rows[:, 1, :], op=ALU.add)

        def transpose_bias():
            bias_bank = banks.tile([P, P], F32, tag="bank")
            nc.tensor.transpose(bias_bank[:], bias_gn[:], ident[:])
            nc.vector.tensor_copy(out=bias_col[:], in_=bias_bank[:, 0:GATE_TILES])
            first_g, last_g = G_TILES
            nc.vector.tensor_scalar(
                out=bias_col[:, first_g : last_g + 1],
                in0=bias_bank[:, first_g : last_g + 1],
                scalar1=2.0,
                scalar2=None,
                op0=ALU.mult,
            )

        def part_x(q):
            rows = slice(2 * q - HALF, 2 * q - HALF + 2)
            nc.gpsimd.tensor_copy(
                out=x_apart[:, rows, :, :],
                in_=x_sb[:, 2 * q : 2 * q + 2, :].bitcast(I32).rearrange("p r (w u) -> p r u w", u=2),
            )

        def transpose_x(q):
            x_bank = banks.tile([P, PER_BANK, P], F32, tag="bank")
            for r in range(2):
                for u in range(2):
                    if 2 * q < HALF:
                        words = x_words[:, 2 * q + r, u : D_IN // 2 : 2]
                    else:
                        words = x_apart[:, 2 * q - HALF + r, u, :].bitcast(F32)
                    nc.tensor.transpose(x_bank[:, 2 * r + u, :], words, ident[:])
            side_by_side = x_grouped[:, 2 * q : 2 * q + 2, :].bitcast(F32).rearrange("p r (b u) -> p r b u", u=2)
            by_word = x_bank[:].rearrange("p (r u) b -> p r b u", u=2)
            if q % 2 == 0:
                nc.vector.tensor_copy(out=side_by_side, in_=by_word)
            else:
                nc.scalar.copy(out=side_by_side, in_=by_word)

        def quantise_x(q):
            cols = slice(2 * q * P, (2 * q + 2) * P)
            nc.vector.quantize_mx(
                out=x_codes[:, cols].bitcast(FP8X4),
                scales=x_plane[:, cols],
                in_=x_grouped[:, 2 * q : 2 * q + 2, :].rearrange("p r c -> p (r c)"),
            )

        def transpose_state(q):
            state_bank = banks.tile([P, PER_BANK, P], F32, tag="bank")
            for which in range(2):
                for r in range(2):
                    nc.tensor.transpose(
                        state_bank[:, 2 * which + r, :], state_words[:, which, 2 * q + r, :], ident[:]
                    )
            nc.vector.tensor_copy(
                out=stateT[:, :, 2 * q : 2 * q + 2, :], in_=state_bank[:].rearrange("p (w r) b -> p w r b", r=2)
            )

        def transpose_weights(j):
            rec_bank = banks.tile([P, PER_BANK, P], F32, tag="bank")
            for t in range(PER_BANK):
                nc.tensor.transpose(rec_bank[:, t, :], rec_words[:, PER_BANK * j + t, :], ident[:])
            if j != 1:
                copy = nc.scalar.copy if j == 0 else nc.vector.tensor_copy
                copy(out=recT[:, j * CHUNK : (j + 1) * CHUNK], in_=rec_bank[:].rearrange("p t n -> p (t n)"))
            else:
                nc.scalar.activation(
                    out=recT_bf[:, 2 * CHUNK : 3 * CHUNK],
                    in_=rec_bank[:, 2:4, :].rearrange("p t n -> p (t n)").bitcast(BF16),
                    func=ACT.Copy,
                    scale=2.0,
                )
                nc.scalar.copy(
                    out=recT[:, CHUNK + 2 * P : 2 * CHUNK], in_=rec_bank[:, 0:2, :].rearrange("p t n -> p (t n)")
                )

        mx_banks = {}

        def mx_pass(half, g):
            rows = slice(half * CHUNK, (half + 1) * CHUNK)
            cols = slice(g * P, (g + 1) * P)
            mx_bank = banks.tile([P, CHUNK], F32, tag="bank")
            mx_banks[g] = mx_bank
            nc.tensor.matmul_mx(
                out=mx_bank[:],
                lhsT=w_words[:, cols].bitcast(FP8X4),
                lhsT_scale=w_plane[:, cols],
                rhs=x_codes[:, rows].bitcast(FP8X4),
                rhs_scale=x_plane[:, rows],
                start=True,
                stop=True,
            )

        def mx_leave(half, g):
            factor = 2.0 if g in G_TILES else 1.0
            if g % 2 == 0:
                nc.vector.tensor_scalar(
                    out=mxT[:, half, g, :],
                    in0=mx_banks[g][:],
                    scalar1=factor,
                    scalar2=bias_col[:, g : g + 1],
                    op0=ALU.mult,
                    op1=ALU.add,
                )
            else:
                nc.scalar.activation(
                    out=mxT[:, half, g, :],
                    in_=mx_banks[g][:],
                    func=ACT.Identity,
                    bias=bias_col[:, g : g + 1],
                    scale=factor,
                )

        def mx_transposed(half, gate_tiles):
            for g in gate_tiles:
                mx_pass(half, g)
                mx_leave(half, g)

        def plain_pass(unit, e, z_bank):
            r, j = unit
            nc.tensor.matmul(
                out=z_bank[:],
                lhsT=stateT_bf[:, j // 2, r, e : 2 * P : 2],
                rhs=recT_bf[:, 2 * j * CHUNK + e : 2 * (j + 1) * CHUNK : 2],
                start=(e == 0),
                stop=False,
            )

        def add_back(unit, t, z_bank):
            r, j = unit
            nc.tensor.matmul(
                out=z_bank[:, t * P : (t + 1) * P],
                lhsT=mxT[:, r // HALF, TILE_ORDER[PER_BANK * j + t], (r % HALF) * P : (r % HALF + 1) * P],
                rhs=ident[:],
                is_transpose=True,
                start=False,
                stop=(t == PER_BANK - 1),
            )

        def cell_state(r, gates):
            m = mask_f[:, r : r + 1]
            res = work.tile([P, 4, HID], F32)
            keep_part = work.tile([P, HID], F32)
            new_part = work.tile([P, HID], F32)
            nc.vector.scalar_tensor_tensor(
                out=keep_part[:], in0=gates[:, 1, :], scalar=m, in1=c_sb[:, r, :], op0=ALU.mult, op1=ALU.mult
            )
            nc.vector.scalar_tensor_tensor(
                out=new_part[:], in0=gates[:, 2, :], scalar=-0.5, in1=gates[:, 0, :], op0=ALU.add, op1=ALU.mult
            )
            return res, keep_part, new_part

        def sum_state(r, res, keep_part, new_part):
            nc.vector.scalar_tensor_tensor(
                out=res[:, 0, :], in0=new_part[:], scalar=mask_2[:, r : r + 1], in1=keep_part[:], op0=ALU.mult, op1=ALU.add
            )
            nc.sync.dma_start(out=out_rows[0][:, r, :], in_=res[:, 0, :])

        def tanh_state(res):
            tanh_c = work.tile([P, HID], F32)
            nc.scalar.activation(out=tanh_c[:], in_=res[:, 0, :], func=ACT.Tanh)
            return tanh_c

        def outputs(r, gates, res, tanh_c, first, last):
            n = last - first + 1
            nc.vector.scalar_tensor_tensor(
                out=res[:, first : last + 1, :],
                in0=gates[:, first + 2 : last + 3, :],
                scalar=mask_f[:, r : r + 1],
                in1=tanh_c[:].unsqueeze(1).to_broadcast([P, n, HID]),
                op0=ALU.mult,
                op1=ALU.mult,
            )
            for k in range(first, last + 1):
                nc.sync.dma_start(out=out_rows[k][:, r, :], in_=res[:, k, :])

        out_rows = [o.rearrange("(p r) c -> p r c", r=ROW_TILES) for o in (out_1, out_0, out_2, out_3)]

        part_x(2)
        part_x(3)
        transpose_x(0)
        add_biases()
        transpose_x(1)
        quantise_x(0)
        quantise_x(1)
        idle_passes(WARM_AGAIN)
        transpose_bias()
        transpose_weights(0)
        mx_transposed(0, range(0, 2 * PER_BANK))
        transpose_state(0)
        transpose_weights(1)
        mx_transposed(0, range(2 * PER_BANK, GATE_TILES))
        transpose_weights(2)
        nc.vector.tensor_copy(out=mask_f[:], in_=mask_bf[:])
        nc.vector.tensor_scalar(out=mask_2[:], in0=mask_bf[:], scalar1=2.0, scalar2=None, op0=ALU.mult)
        units = [divmod(k, N_CHUNKS) for k in range(UNITS)]
        late = range(LAST - 2, LAST)
        for r in late:
            units.remove((r, 2))
            units.insert(-1, (r, 2))
        behind = {
            1: [(transpose_state, 1)],
            2: [(transpose_x, 2)],
            3: [(transpose_x, 3), (quantise_x, 2)],
            4: [(quantise_x, 3)],
            6: [(transpose_state, 2)],
            12: [(transpose_state, 3)],
        }
        pairs = {N_CHUNKS * 2 + 1 + i: i for i in range(GATE_TILES // 2)}
        z_banks, gates, res, tanh = {}, {}, {}, {}
        for k in range(UNITS + 1):
            if k < UNITS:
                z_bank = banks.tile([P, CHUNK], F32, tag="bank")
                z_banks[k] = z_bank
            for e in range(2):
                if k < UNITS:
                    plain_pass(units[k], e, z_banks[k])
                if k > 0:
                    add_back(units[k - 1], 2 * e, z_banks[k - 1])
                    add_back(units[k - 1], 2 * e + 1, z_banks[k - 1])
            if k == 0:
                continue
            if k in pairs:
                for g in range(2):
                    mx_pass(1, 2 * pairs[k] + g)
                mx_leave(1, 2 * pairs[k])
            r, j = units[k - 1]
            z = z_banks[k - 1]
            if j == 0:
                gates_r = work.tile([P, 6, HID], F32)
                gates[r] = gates_r
                nc.scalar.activation(out=gates[r][:, 0:2, :].rearrange("p g c -> p (g c)"), in_=z[:], func=ACT.Sigmoid)
            if j == 1:
                if r in (0, LAST):
                    nc.scalar.activation(out=gates[r][:, 2, :], in_=z[:, 0:HID], func=ACT.Sigmoid)
                    nc.scalar.activation(out=gates[r][:, 3, :], in_=z[:, HID : 2 * HID], func=ACT.Sigmoid)
                else:
                    nc.scalar.activation(
                        out=gates[r][:, 2:4, :].rearrange("p g c -> p (g c)"), in_=z[:], func=ACT.Sigmoid
                    )
                res[r], keep_part, new_part = cell_state(r, gates[r])
                if r == LAST:
                    sum_state(r, res[r], keep_part, new_part)
                if r > 0:
                    tanh[r - 1] = tanh_state(res[r - 1])
                    outputs(r - 1, gates[r - 1], res[r - 1], tanh[r - 1], 1, 1 if r - 1 in late else 3)
                if r < LAST:
                    sum_state(r, res[r], keep_part, new_part)
            if j == 2 and r == LAST:
                for g in range(2):
                    nc.scalar.activation(out=gates[r][:, 4 + g, :], in_=z[:, g * HID : (g + 1) * HID], func=ACT.Sigmoid)
                    outputs(r, gates[r], res[r], tanh[r], 2 + g, 2 + g)
            if j == 2 and r < LAST:
                nc.scalar.activation(out=gates[r][:, 4:6, :].rearrange("p g c -> p (g c)"), in_=z[:], func=ACT.Sigmoid)
                if r in late:
                    outputs(r, gates[r], res[r], tanh[r], 2, 3)
                if r == late[-1]:
                    tanh[LAST] = tanh_state(res[LAST])
                    outputs(LAST, gates[LAST], res[LAST], tanh[LAST], 1, 1)
            for job, which in behind.get(k, ()):
                job(which)
            if k in pairs:
                mx_leave(1, 2 * pairs[k] + 1)
